import numpy as np
import ml_dtypes

BF16 = ml_dtypes.bfloat16


def bf(x):
    return np.asarray(x, np.float32).astype(BF16)


def f32(x):
    return np.asarray(x, np.float32)


def f64(x):
    return np.asarray(x).astype(np.float64)


def striped(idx):
    return np.tile(idx.reshape(-1, 16).T, (8, 1))


S, D, H, DK, E, N = 2048, 128, 2, 128, 3, 1024


def draw_w():
    return bf(np.random.standard_normal((D, H * DK)) / np.sqrt(D))


def qk_score(z, idx, wq, wk):
    qry = (z[idx] @ wq).reshape(N, H, DK)
    key = (z @ wk).reshape(S, H, DK)
    return np.einsum("shd,jhd->hsj", key, qry) / np.sqrt(DK)


def setup_inputs():
    return {"z": bf(np.random.standard_normal((S, D))), "wq_seq": draw_w(), "wk_seq": draw_w(), "wq_exp": draw_w(), "wk_exp": draw_w(), "wq_txt": draw_w(), "wk_txt": draw_w(), "gate_w": f32(np.eye(E)[None] + 0.1 * np.random.standard_normal((H, E, E))), "gate_b": f32(0.3 * np.random.standard_normal((H, E))), "offs": striped(np.random.permutation(S)[:N])}


def reference(z, wq_seq, wk_seq, wq_exp, wk_exp, wq_txt, wk_txt, gate_w, gate_b, offs):
    idx = offs[:16].T.reshape(-1)
    zz = f64(z)
    sc = np.stack([qk_score(zz, idx, f64(wq_seq), f64(wk_seq)), qk_score(zz, idx, f64(wq_exp), f64(wk_exp)), qk_score(zz, idx, f64(wq_txt), f64(wk_txt))])
    gw, gb = f64(gate_w), f64(gate_b)
    acc = np.zeros((S, N))
    for h in range(H):
        logits = np.einsum("esj,ef->fsj", sc[:, h], gw[h]) + gb[h][:, None, None]
        ex = np.exp(logits - logits.max(axis=0))
        acc += (ex * sc[:, h]).sum(axis=0) / ex.sum(axis=0)
    return acc / H

@@ -1,0 +1,222 @@
+import math
+
+import concourse.mybir as mybir
+from concourse.masks import make_identity
+
+S, D, H, DK, E, N = 2048, 128, 2, 128, 3, 1024
+P = 128
+BLOCKS = S // P
+PIECE = 512
+PIECES = N // PIECE
+BATCH = 4
+
+FLOPS = 2 * (N + S) * D * H * DK * E + 2 * S * N * DK * H * E
+
+BF16, F32, U16 = mybir.dt.bfloat16, mybir.dt.float32, mybir.dt.uint16
+MULT, ADD = mybir.AluOpType.mult, mybir.AluOpType.add
+EXP = mybir.ActivationFunctionType.Exp
+TANH = mybir.ActivationFunctionType.Tanh
+ROOT = mybir.ActivationFunctionType.Abs_reciprocal_sqrt
+
+GAPS = ((1, 0), (2, 0), (2, 1))
+SWING = {1: -0.5 / H, 2: 0.5 / H}
+RISE = {0: -1.0 / H, 1: 0.5 / H, 2: 0.5 / H}
+FIRST = {0: 1.0 / H}
+
+
+def piece_columns(piece):
+    return slice(piece * PIECE, (piece + 1) * PIECE)
+
+
+def tile_multiheadefralayer_nomp_b_kernel(
+    tc, z, wq_seq, wk_seq, wq_exp, wk_exp, wq_txt, wk_txt, gate_w, gate_b, offs, out
+):
+    nc = tc.nc
+    inv_sqrt_dk = 1.0 / math.sqrt(DK)
+
+    with (
+        tc.tile_pool(name="held", bufs=1) as held,
+        tc.tile_pool(name="denoms", bufs=BATCH + 1) as denoms,
+        tc.tile_pool(name="spreads", bufs=2 * BATCH) as spreads,
+        tc.tile_pool(name="roots", bufs=BATCH + 1) as roots,
+        tc.tile_pool(name="work", bufs=3) as work,
+    ):
+        offsets = held.tile([P, N // 16], U16, name="offsets")
+        nc.sync.dma_start(offsets[:], offs)
+
+        z_rows = held.tile([P, BLOCKS, D], BF16, name="z_rows")
+        z_blocks = z.rearrange("(b p) c -> p b c", p=P)
+        half = BLOCKS // 2
+        nc.sync.dma_start(z_rows[:, :half, :], z_blocks[:, :half, :])
+        nc.scalar.dma_start(z_rows[:, half:, :], z_blocks[:, half:, :])
+
+        wq = [held.tile([D, H * DK], BF16, name=f"wq{e}") for e in range(E)]
+        wk = [held.tile([D, H * DK], BF16, name=f"wk{e}") for e in range(E)]
+        for e, (wq_dram, wk_dram) in enumerate(((wq_seq, wk_seq), (wq_exp, wk_exp), (wq_txt, wk_txt))):
+            nc.gpsimd.dma_start(wk[e][:], wk_dram)
+            nc.gpsimd.dma_start(wq[e][:], wq_dram)
+
+        gate = held.tile([P, H * E * E], F32, name="gate")
+        nc.scalar.dma_start(gate[:], gate_w.rearrange("h e f -> (h e f)").partition_broadcast(P))
+        gate_bias = held.tile([P, H * E], F32, name="gate_bias")
+        nc.scalar.dma_start(gate_bias[:], gate_b.rearrange("h f -> (h f)").partition_broadcast(P))
+
+        identity = held.tile([P, P], BF16, name="identity")
+        make_identity(nc, identity[:])
+        one = held.tile([P, 1], F32, name="one")
+        nc.vector.memset(one[:], 1.0)
+
+        gate_by_f = gate[:].rearrange("p (a f) -> p a f", f=E)
+        bias_by_f = gate_bias[:].rearrange("p (h f) -> p h f", f=E)
+        gap_weight = held.tile([P, len(GAPS), H * E], F32, name="gap_weight")
+        gap_bias = held.tile([P, len(GAPS), H], F32, name="gap_bias")
+        for g, (high, low) in enumerate(GAPS):
+            nc.vector.tensor_sub(gap_weight[:, g, :], gate_by_f[:, :, high], gate_by_f[:, :, low])
+            nc.vector.tensor_sub(gap_bias[:, g, :], bias_by_f[:, :, high], bias_by_f[:, :, low])
+        nc.vector.tensor_scalar_mul(gap_bias[:, 2, :], gap_bias[:, 2, :], 0.5)
+
+        table = held.tile([D, S], BF16, name="table")
+        qry = [[held.tile([DK, N], BF16, name=f"qry{e}{h}") for h in range(H)] for e in range(E)]
+
+        with (
+            tc.psum_pool(name="flip_psum", bufs=1) as flip_psum,
+            tc.psum_pool(name="acc_psum", bufs=4) as acc_psum,
+        ):
+            per_bank = 1024 // P
+            for bank in range(BLOCKS // per_bank):
+                flipped = flip_psum.tile([D, per_bank * P], BF16, name=f"flipped{bank}")
+                for i in range(per_bank):
+                    nc.tensor.transpose(flipped[:, i * P : (i + 1) * P], z_rows[:, bank * per_bank + i, :], identity[:])
+                columns = slice(bank * per_bank * P, (bank + 1) * per_bank * P)
+                if bank % 2 == 0:
+                    nc.vector.tensor_copy(table[:, columns], flipped[:])
+                else:
+                    nc.scalar.copy(table[:, columns], flipped[:])
+
+            wk_t = flip_psum.tile([DK, E * H * D], BF16, name="wk_t")
+            for e in range(E):
+                for h in range(H):
+                    block = e * H + h
+                    nc.tensor.transpose(wk_t[:, block * D : (block + 1) * D], wk[e][:, h * DK : (h + 1) * DK], identity[:])
+
+            turn = 0
+            for e in range(E):
+                for h in range(H):
+                    for piece in range(PIECES):
+                        acc = acc_psum.tile([DK, PIECE], F32, name="acc")
+                        looked_up = table[:].indirect(offsets[:, piece * (PIECE // 16) : (piece + 1) * (PIECE // 16)])
+                        nc.tensor.matmul(acc[:], wq[e][:, h * DK : (h + 1) * DK], looked_up, start=True, stop=True)
+                        if turn % 2 == 0:
+                            nc.vector.tensor_copy(qry[e][h][:, piece_columns(piece)], acc[:])
+                        else:
+                            nc.scalar.copy(qry[e][h][:, piece_columns(piece)], acc[:])
+                        turn += 1
+
+            def fold(name, terms):
+                mixers = []
+                for h, e, column, number in terms:
+                    mixer = held.tile([DK, D], BF16, name=f"{name}_mixer{h}{e}")
+                    block = e * H + h
+                    source = wk_t[:, block * D : (block + 1) * D]
+                    if column is None:
+                        nc.vector.tensor_scalar_mul(mixer[:], source, number)
+                    else:
+                        nc.vector.tensor_scalar(mixer[:], source, column, number, MULT, MULT)
+                    mixers.append(mixer)
+                folded = held.tile([D, N], BF16, name=name)
+                for piece in range(PIECES):
+                    acc = acc_psum.tile([D, PIECE], F32, name="acc")
+                    for i, (h, e, column, number) in enumerate(terms):
+                        nc.tensor.matmul(
+                            acc[:], mixers[i][:], qry[e][h][:, piece_columns(piece)],
+                            start=(i == 0), stop=(i == len(terms) - 1),
+                        )
+                    if piece % 2 == 0:
+                        nc.vector.tensor_copy(folded[:, piece_columns(piece)], acc[:])
+                    else:
+                        nc.scalar.copy(folded[:, piece_columns(piece)], acc[:])
+                return folded
+
+            def fixed(h, combination):
+                return [(h, e, None, a * inv_sqrt_dk) for e, a in combination.items()]
+
+            def gated(h, g):
+                return [(h, e, gap_weight[:, g, h * E + e : h * E + e + 1], inv_sqrt_dk) for e in range(E)]
+
+            fold_gap = [[fold(f"fold_gap{g}{h}", gated(h, g)) for g in range(len(GAPS))] for h in range(H)]
+            fold_swing = [fold(f"fold_swing{h}", fixed(h, SWING)) for h in range(H)]
+            fold_rise = [fold(f"fold_rise{h}", fixed(h, RISE)) for h in range(H)]
+            fold_first = fold("fold_first", fixed(0, FIRST) + fixed(1, FIRST))
+
+        with (
+            tc.psum_pool(name="gap_psum", bufs=3) as gap_psum,
+            tc.psum_pool(name="score_psum", bufs=3) as score_psum,
+            tc.psum_pool(name="first_psum", bufs=2) as first_psum,
+        ):
+            denom_of, spread_of, root_of = {}, {}, {}
+
+            def genes(blk):
+                return table[:, blk * P : (blk + 1) * P]
+
+            def against_genes(blk, folded, pool, tag):
+                product = pool.tile([P, N], BF16, name=tag)
+                for piece in range(PIECES):
+                    nc.tensor.matmul(
+                        product[:, piece_columns(piece)], genes(blk), folded[:, piece_columns(piece)],
+                        start=True, stop=True,
+                    )
+                return product
+
+            def mix(blk):
+                denom = denoms.tile([P, H * N], BF16, name="denom")
+                spread = spreads.tile([P, H * N], BF16, name="spread")
+                for h in range(H):
+                    head = slice(h * N, (h + 1) * N)
+                    gap21 = against_genes(blk, fold_gap[h][2], gap_psum, "gap")
+                    tanh21 = work.tile([P, N], BF16, name="tanh21")
+                    nc.scalar.activation(tanh21[:], gap21[:], TANH, bias=gap_bias[:, 2, h : h + 1], scale=0.5)
+                    gap10 = against_genes(blk, fold_gap[h][0], gap_psum, "gap")
+                    exp10 = work.tile([P, N], BF16, name="exp10")
+                    nc.scalar.activation(exp10[:], gap10[:], EXP, bias=gap_bias[:, 0, h : h + 1])
+                    gap20 = against_genes(blk, fold_gap[h][1], gap_psum, "gap")
+                    exp20 = work.tile([P, N], BF16, name="exp20")
+                    nc.scalar.activation(exp20[:], gap20[:], EXP, bias=gap_bias[:, 1, h : h + 1])
+
+                    swing = against_genes(blk, fold_swing[h], score_psum, "score")
+                    swung = work.tile([P, N], BF16, name="swung")
+                    nc.vector.tensor_mul(swung[:], swing[:], tanh21[:])
+                    rise = against_genes(blk, fold_rise[h], score_psum, "score")
+                    nc.vector.tensor_add(spread[:, head], rise[:], swung[:])
+                    nc.vector.tensor_add(denom[:, head], exp10[:], exp20[:])
+                denom_of[blk], spread_of[blk] = denom, spread
+
+            def invert(blk):
+                root = roots.tile([P, H * N], BF16, name="root")
+                nc.scalar.activation(root[:], denom_of[blk][:], ROOT, bias=one[:, 0:1])
+                root_of[blk] = root
+
+            def finish(blk):
+                alpha0 = work.tile([P, H * N], BF16, name="alpha0")
+                nc.vector.tensor_mul(alpha0[:], root_of[blk][:], root_of[blk][:])
+                others = work.tile([P, H * N], BF16, name="others")
+                nc.vector.tensor_scalar(others[:], alpha0[:], -1.0, 1.0, MULT, ADD)
+                gain = work.tile([P, H * N], BF16, name="gain")
+                nc.vector.tensor_mul(gain[:], others[:], spread_of[blk][:])
+                both = work.tile([P, N], BF16, name="both")
+                nc.vector.tensor_add(both[:], gain[:, :N], gain[:, N:])
+                result = work.tile([P, N], F32, name="result")
+                for piece in range(PIECES):
+                    first = first_psum.tile([P, PIECE], F32, name="first")
+                    nc.tensor.matmul(first[:], genes(blk), fold_first[:, piece_columns(piece)], start=True, stop=True)
+                    nc.vector.tensor_add(result[:, piece_columns(piece)], first[:], both[:, piece_columns(piece)])
+                nc.sync.dma_start(out[blk * P : (blk + 1) * P, :], result[:])
+
+            for start in range(0, BLOCKS, BATCH):
+                for blk in range(start, start + BATCH):
+                    mix(blk)
+                    if start > 0:
+                        finish(blk - BATCH)
+                for blk in range(start, start + BATCH):
+                    invert(blk)
+            for blk in range(BLOCKS - BATCH, BLOCKS):
+                finish(blk)

@@ -9,11 +9,12 @@ BLOCKS = S // P
 PIECE = 512
 PIECES = N // PIECE
 BATCH = 4
+CAP = 2.0 ** 30
 
 FLOPS = 2 * (N + S) * D * H * DK * E + 2 * S * N * DK * H * E
 
 BF16, F32, U16 = mybir.dt.bfloat16, mybir.dt.float32, mybir.dt.uint16
-MULT, ADD = mybir.AluOpType.mult, mybir.AluOpType.add
+MULT, ADD, MIN = mybir.AluOpType.mult, mybir.AluOpType.add, mybir.AluOpType.min
 EXP = mybir.ActivationFunctionType.Exp
 TANH = mybir.ActivationFunctionType.Tanh
 ROOT = mybir.ActivationFunctionType.Abs_reciprocal_sqrt
@@ -36,42 +37,45 @@ def tile_multiheadefralayer_nomp_b_kernel(
 
     with (
         tc.tile_pool(name="held", bufs=1) as held,
-        tc.tile_pool(name="denoms", bufs=BATCH + 1) as denoms,
+        tc.tile_pool(name="batches", bufs=2) as batches,
         tc.tile_pool(name="spreads", bufs=2 * BATCH) as spreads,
-        tc.tile_pool(name="roots", bufs=BATCH + 1) as roots,
-        tc.tile_pool(name="work", bufs=3) as work,
+        tc.tile_pool(name="oweds", bufs=2 * BATCH) as oweds,
+        tc.tile_pool(name="narrow", bufs=3) as narrow,
+        tc.tile_pool(name="wide", bufs=2) as wide,
     ):
+        identity = held.tile([P, P], BF16, name="identity")
+        make_identity(nc, identity[:])
+        minus_identity = held.tile([P, P], BF16, name="minus_identity")
+        nc.gpsimd.tensor_scalar_mul(minus_identity[:], identity[:], -1.0)
+
         offsets = held.tile([P, N // 16], U16, name="offsets")
         nc.sync.dma_start(offsets[:], offs)
 
         z_rows = held.tile([P, BLOCKS, D], BF16, name="z_rows")
         z_blocks = z.rearrange("(b p) c -> p b c", p=P)
-        half = BLOCKS // 2
-        nc.sync.dma_start(z_rows[:, :half, :], z_blocks[:, :half, :])
-        nc.scalar.dma_start(z_rows[:, half:, :], z_blocks[:, half:, :])
+        quarter = BLOCKS // 4
+        for i in range(4):
+            queue = nc.sync if i % 2 == 0 else nc.scalar
+            queue.dma_start(z_rows[:, i * quarter : (i + 1) * quarter, :], z_blocks[:, i * quarter : (i + 1) * quarter, :])
 
         wq = [held.tile([D, H * DK], BF16, name=f"wq{e}") for e in range(E)]
         wk = [held.tile([D, H * DK], BF16, name=f"wk{e}") for e in range(E)]
         for e, (wq_dram, wk_dram) in enumerate(((wq_seq, wk_seq), (wq_exp, wk_exp), (wq_txt, wk_txt))):
-            nc.gpsimd.dma_start(wk[e][:], wk_dram)
-            nc.gpsimd.dma_start(wq[e][:], wq_dram)
+            nc.sync.dma_start(wq[e][:], wq_dram)
+            nc.scalar.dma_start(wk[e][:], wk_dram)
 
         gate = held.tile([P, H * E * E], F32, name="gate")
         nc.scalar.dma_start(gate[:], gate_w.rearrange("h e f -> (h e f)").partition_broadcast(P))
         gate_bias = held.tile([P, H * E], F32, name="gate_bias")
         nc.scalar.dma_start(gate_bias[:], gate_b.rearrange("h f -> (h f)").partition_broadcast(P))
 
-        identity = held.tile([P, P], BF16, name="identity")
-        make_identity(nc, identity[:])
-        one = held.tile([P, 1], F32, name="one")
-        nc.vector.memset(one[:], 1.0)
-
         gate_by_f = gate[:].rearrange("p (a f) -> p a f", f=E)
         bias_by_f = gate_bias[:].rearrange("p (h f) -> p h f", f=E)
-        gap_weight = held.tile([P, len(GAPS), H * E], F32, name="gap_weight")
+        gap_weight = held.tile([P, 2, H * E], F32, name="gap_weight")
         gap_bias = held.tile([P, len(GAPS), H], F32, name="gap_bias")
         for g, (high, low) in enumerate(GAPS):
-            nc.vector.tensor_sub(gap_weight[:, g, :], gate_by_f[:, :, high], gate_by_f[:, :, low])
+            if g < 2:
+                nc.vector.tensor_sub(gap_weight[:, g, :], gate_by_f[:, :, high], gate_by_f[:, :, low])
             nc.vector.tensor_sub(gap_bias[:, g, :], bias_by_f[:, :, high], bias_by_f[:, :, low])
         nc.vector.tensor_scalar_mul(gap_bias[:, 2, :], gap_bias[:, 2, :], 0.5)
 
@@ -79,12 +83,13 @@ def tile_multiheadefralayer_nomp_b_kernel(
         qry = [[held.tile([DK, N], BF16, name=f"qry{e}{h}") for h in range(H)] for e in range(E)]
 
         with (
-            tc.psum_pool(name="flip_psum", bufs=1) as flip_psum,
-            tc.psum_pool(name="acc_psum", bufs=4) as acc_psum,
+            tc.psum_pool(name="gap_psum", bufs=3) as gap_psum,
+            tc.psum_pool(name="score_psum", bufs=2) as score_psum,
+            tc.psum_pool(name="sum_psum", bufs=3) as sum_psum,
         ):
             per_bank = 1024 // P
             for bank in range(BLOCKS // per_bank):
-                flipped = flip_psum.tile([D, per_bank * P], BF16, name=f"flipped{bank}")
+                flipped = gap_psum.tile([D, per_bank * P], BF16, name="gap")
                 for i in range(per_bank):
                     nc.tensor.transpose(flipped[:, i * P : (i + 1) * P], z_rows[:, bank * per_bank + i, :], identity[:])
                 columns = slice(bank * per_bank * P, (bank + 1) * per_bank * P)
@@ -93,17 +98,19 @@ def tile_multiheadefralayer_nomp_b_kernel(
                 else:
                     nc.scalar.copy(table[:, columns], flipped[:])
 
-            wk_t = flip_psum.tile([DK, E * H * D], BF16, name="wk_t")
+            wk_flipped = score_psum.tile([DK, E * H * D], BF16, name="score")
             for e in range(E):
                 for h in range(H):
                     block = e * H + h
-                    nc.tensor.transpose(wk_t[:, block * D : (block + 1) * D], wk[e][:, h * DK : (h + 1) * DK], identity[:])
+                    nc.tensor.transpose(wk_flipped[:, block * D : (block + 1) * D], wk[e][:, h * DK : (h + 1) * DK], identity[:])
+            wk_t = held.tile([DK, E * H * D], BF16, name="wk_t")
+            nc.vector.tensor_copy(wk_t[:], wk_flipped[:])
 
             turn = 0
-            for e in range(E):
-                for h in range(H):
+            for h in range(H):
+                for e in range(E):
                     for piece in range(PIECES):
-                        acc = acc_psum.tile([DK, PIECE], F32, name="acc")
+                        acc = sum_psum.tile([DK, PIECE], F32, name="sum")
                         looked_up = table[:].indirect(offsets[:, piece * (PIECE // 16) : (piece + 1) * (PIECE // 16)])
                         nc.tensor.matmul(acc[:], wq[e][:, h * DK : (h + 1) * DK], looked_up, start=True, stop=True)
                         if turn % 2 == 0:
@@ -125,16 +132,13 @@ def tile_multiheadefralayer_nomp_b_kernel(
                     mixers.append(mixer)
                 folded = held.tile([D, N], BF16, name=name)
                 for piece in range(PIECES):
-                    acc = acc_psum.tile([D, PIECE], F32, name="acc")
+                    acc = sum_psum.tile([D, PIECE], F32, name="sum")
                     for i, (h, e, column, number) in enumerate(terms):
                         nc.tensor.matmul(
                             acc[:], mixers[i][:], qry[e][h][:, piece_columns(piece)],
                             start=(i == 0), stop=(i == len(terms) - 1),
                         )
-                    if piece % 2 == 0:
-                        nc.vector.tensor_copy(folded[:, piece_columns(piece)], acc[:])
-                    else:
-                        nc.scalar.copy(folded[:, piece_columns(piece)], acc[:])
+                    nc.vector.tensor_copy(folded[:, piece_columns(piece)], acc[:])
                 return folded
 
             def fixed(h, combination):
@@ -143,17 +147,21 @@ def tile_multiheadefralayer_nomp_b_kernel(
             def gated(h, g):
                 return [(h, e, gap_weight[:, g, h * E + e : h * E + e + 1], inv_sqrt_dk) for e in range(E)]
 
-            fold_gap = [[fold(f"fold_gap{g}{h}", gated(h, g)) for g in range(len(GAPS))] for h in range(H)]
-            fold_swing = [fold(f"fold_swing{h}", fixed(h, SWING)) for h in range(H)]
-            fold_rise = [fold(f"fold_rise{h}", fixed(h, RISE)) for h in range(H)]
-            fold_first = fold("fold_first", fixed(0, FIRST) + fixed(1, FIRST))
+            folds = {}
 
-        with (
-            tc.psum_pool(name="gap_psum", bufs=3) as gap_psum,
-            tc.psum_pool(name="score_psum", bufs=3) as score_psum,
-            tc.psum_pool(name="first_psum", bufs=2) as first_psum,
-        ):
-            denom_of, spread_of, root_of = {}, {}, {}
+            def folded_query(name, terms):
+                if name not in folds:
+                    folds[name] = fold(name, terms)
+                return folds[name]
+
+            def fold_of_difference(h):
+                name = f"fold_gap2{h}"
+                if name not in folds:
+                    folds[name] = held.tile([D, N], BF16, name=name)
+                    nc.vector.tensor_sub(folds[name][:], folds[f"fold_gap1{h}"][:], folds[f"fold_gap0{h}"][:])
+                return folds[name]
+
+            spread_of, owed_of = {}, {}
 
             def genes(blk):
                 return table[:, blk * P : (blk + 1) * P]
@@ -167,56 +175,64 @@ def tile_multiheadefralayer_nomp_b_kernel(
                     )
                 return product
 
-            def mix(blk):
-                denom = denoms.tile([P, H * N], BF16, name="denom")
+            def mix(blk, square):
+                denom = wide.tile([P, H * N], BF16, name="denom")
                 spread = spreads.tile([P, H * N], BF16, name="spread")
                 for h in range(H):
                     head = slice(h * N, (h + 1) * N)
-                    gap21 = against_genes(blk, fold_gap[h][2], gap_psum, "gap")
-                    tanh21 = work.tile([P, N], BF16, name="tanh21")
-                    nc.scalar.activation(tanh21[:], gap21[:], TANH, bias=gap_bias[:, 2, h : h + 1], scale=0.5)
-                    gap10 = against_genes(blk, fold_gap[h][0], gap_psum, "gap")
-                    exp10 = work.tile([P, N], BF16, name="exp10")
+                    gap10 = against_genes(blk, folded_query(f"fold_gap0{h}", gated(h, 0)), gap_psum, "gap")
+                    exp10 = narrow.tile([P, N], BF16, name="exp10")
                     nc.scalar.activation(exp10[:], gap10[:], EXP, bias=gap_bias[:, 0, h : h + 1])
-                    gap20 = against_genes(blk, fold_gap[h][1], gap_psum, "gap")
-                    exp20 = work.tile([P, N], BF16, name="exp20")
+                    gap20 = against_genes(blk, folded_query(f"fold_gap1{h}", gated(h, 1)), gap_psum, "gap")
+                    exp20 = narrow.tile([P, N], BF16, name="exp20")
                     nc.scalar.activation(exp20[:], gap20[:], EXP, bias=gap_bias[:, 1, h : h + 1])
+                    nc.gpsimd.tensor_add(denom[:, head], exp10[:], exp20[:])
+                    gap21 = against_genes(blk, fold_of_difference(h), gap_psum, "gap")
+                    tanh21 = narrow.tile([P, N], BF16, name="tanh21")
+                    nc.scalar.activation(tanh21[:], gap21[:], TANH, bias=gap_bias[:, 2, h : h + 1], scale=0.5)
 
-                    swing = against_genes(blk, fold_swing[h], score_psum, "score")
-                    swung = work.tile([P, N], BF16, name="swung")
+                    swing = against_genes(blk, folded_query(f"fold_swing{h}", fixed(h, SWING)), score_psum, "score")
+                    swung = narrow.tile([P, N], BF16, name="swung")
                     nc.vector.tensor_mul(swung[:], swing[:], tanh21[:])
-                    rise = against_genes(blk, fold_rise[h], score_psum, "score")
+                    rise = against_genes(blk, folded_query(f"fold_rise{h}", fixed(h, RISE)), score_psum, "score")
                     nc.vector.tensor_add(spread[:, head], rise[:], swung[:])
-                    nc.vector.tensor_add(denom[:, head], exp10[:], exp20[:])
-                denom_of[blk], spread_of[blk] = denom, spread
 
-            def invert(blk):
-                root = roots.tile([P, H * N], BF16, name="root")
-                nc.scalar.activation(root[:], denom_of[blk][:], ROOT, bias=one[:, 0:1])
-                root_of[blk] = root
+                capped = wide.tile([P, H * N], BF16, name="capped")
+                nc.vector.tensor_scalar(capped[:], denom[:], 1.0, CAP, ADD, MIN)
+                product = narrow.tile([P, N], BF16, name="product")
+                nc.vector.tensor_mul(product[:], capped[:, :N], capped[:, N:])
+                nc.vector.tensor_mul(square, product[:], product[:])
+                weighted = wide.tile([P, H * N], BF16, name="weighted")
+                nc.vector.tensor_mul(weighted[:, :N], capped[:, N:], spread[:, :N])
+                nc.vector.tensor_mul(weighted[:, N:], capped[:, :N], spread[:, N:])
+                owed = oweds.tile([P, N], BF16, name="owed")
+                nc.vector.tensor_add(owed[:], weighted[:, :N], weighted[:, N:])
+                spread_of[blk], owed_of[blk] = spread, owed
 
-            def finish(blk):
-                alpha0 = work.tile([P, H * N], BF16, name="alpha0")
-                nc.vector.tensor_mul(alpha0[:], root_of[blk][:], root_of[blk][:])
-                others = work.tile([P, H * N], BF16, name="others")
-                nc.vector.tensor_scalar(others[:], alpha0[:], -1.0, 1.0, MULT, ADD)
-                gain = work.tile([P, H * N], BF16, name="gain")
-                nc.vector.tensor_mul(gain[:], others[:], spread_of[blk][:])
-                both = work.tile([P, N], BF16, name="both")
-                nc.vector.tensor_add(both[:], gain[:, :N], gain[:, N:])
-                result = work.tile([P, N], F32, name="result")
+            def finish(blk, inverse):
+                back = narrow.tile([P, N], BF16, name="back")
+                nc.vector.tensor_mul(back[:], inverse, owed_of[blk][:])
+                fold_first = folded_query("fold_first", fixed(0, FIRST) + fixed(1, FIRST))
+                result = wide.tile([P, N], F32, name="result")
                 for piece in range(PIECES):
-                    first = first_psum.tile([P, PIECE], F32, name="first")
-                    nc.tensor.matmul(first[:], genes(blk), fold_first[:, piece_columns(piece)], start=True, stop=True)
-                    nc.vector.tensor_add(result[:, piece_columns(piece)], first[:], both[:, piece_columns(piece)])
+                    total = sum_psum.tile([P, PIECE], F32, name="sum")
+                    nc.tensor.matmul(total[:], genes(blk), fold_first[:, piece_columns(piece)], start=True, stop=False)
+                    for h in range(H):
+                        columns = slice(h * N + piece * PIECE, h * N + (piece + 1) * PIECE)
+                        nc.tensor.matmul(total[:], identity[:], spread_of[blk][:, columns], start=False, stop=False)
+                    nc.tensor.matmul(total[:], minus_identity[:], back[:, piece_columns(piece)], start=False, stop=True)
+                    nc.vector.tensor_copy(result[:, piece_columns(piece)], total[:])
                 nc.sync.dma_start(out[blk * P : (blk + 1) * P, :], result[:])
 
+            inverse_before = None
             for start in range(0, BLOCKS, BATCH):
-                for blk in range(start, start + BATCH):
-                    mix(blk)
-                    if start > 0:
-                        finish(blk - BATCH)
-                for blk in range(start, start + BATCH):
-                    invert(blk)
-            for blk in range(BLOCKS - BATCH, BLOCKS):
-                finish(blk)
+                squares = batches.tile([P, BATCH * N], BF16, name="squares")
+                for i in range(BATCH):
+                    mix(start + i, squares[:, i * N : (i + 1) * N])
+                    if inverse_before is not None:
+                        finish(start - BATCH + i, inverse_before[:, i * N : (i + 1) * N])
+                inverses = batches.tile([P, BATCH * N], BF16, name="inverses")
+                nc.scalar.activation(inverses[:], squares[:], ROOT)
+                inverse_before = inverses
+            for i in range(BATCH):
+                finish(BLOCKS - BATCH + i, inverse_before[:, i * N : (i + 1) * N])

@@ -186,7 +186,7 @@ def tile_multiheadefralayer_nomp_b_kernel(
                     gap20 = against_genes(blk, folded_query(f"fold_gap1{h}", gated(h, 1)), gap_psum, "gap")
                     exp20 = narrow.tile([P, N], BF16, name="exp20")
                     nc.scalar.activation(exp20[:], gap20[:], EXP, bias=gap_bias[:, 1, h : h + 1])
-                    nc.gpsimd.tensor_add(denom[:, head], exp10[:], exp20[:])
+                    nc.vector.tensor_add(denom[:, head], exp10[:], exp20[:])
                     gap21 = against_genes(blk, fold_of_difference(h), gap_psum, "gap")
                     tanh21 = narrow.tile([P, N], BF16, name="tanh21")
                     nc.scalar.activation(tanh21[:], gap21[:], TANH, bias=gap_bias[:, 2, h : h + 1], scale=0.5)

@@ -37,6 +37,9 @@ def tile_multiheadefralayer_nomp_b_kernel(
 
     with (
         tc.tile_pool(name="held", bufs=1) as held,
+        tc.tile_pool(name="tanhs", bufs=3 * H) as tanhs,
+        tc.tile_pool(name="cappeds", bufs=3) as cappeds,
+        tc.tile_pool(name="results", bufs=4) as results,
         tc.tile_pool(name="batches", bufs=2) as batches,
         tc.tile_pool(name="spreads", bufs=2 * BATCH) as spreads,
         tc.tile_pool(name="oweds", bufs=2 * BATCH) as oweds,
@@ -161,7 +164,7 @@ def tile_multiheadefralayer_nomp_b_kernel(
                     nc.vector.tensor_sub(folds[name][:], folds[f"fold_gap1{h}"][:], folds[f"fold_gap0{h}"][:])
                 return folds[name]
 
-            spread_of, owed_of = {}, {}
+            spread_of, owed_of, tanh_of, capped_of = {}, {}, {}, {}
 
             def genes(blk):
                 return table[:, blk * P : (blk + 1) * P]
@@ -175,36 +178,40 @@ def tile_multiheadefralayer_nomp_b_kernel(
                     )
                 return product
 
-            def mix(blk, square):
-                denom = wide.tile([P, H * N], BF16, name="denom")
-                spread = spreads.tile([P, H * N], BF16, name="spread")
+            def gates(blk, square):
+                exp10 = wide.tile([P, H * N], BF16, name="exp10")
+                exp20 = wide.tile([P, H * N], BF16, name="exp20")
+                tanh_of[blk] = []
                 for h in range(H):
-                    head = slice(h * N, (h + 1) * N)
+                    across = slice((H - 1 - h) * N, (H - h) * N)
                     gap10 = against_genes(blk, folded_query(f"fold_gap0{h}", gated(h, 0)), gap_psum, "gap")
-                    exp10 = narrow.tile([P, N], BF16, name="exp10")
-                    nc.scalar.activation(exp10[:], gap10[:], EXP, bias=gap_bias[:, 0, h : h + 1])
+                    nc.scalar.activation(exp10[:, across], gap10[:], EXP, bias=gap_bias[:, 0, h : h + 1])
                     gap20 = against_genes(blk, folded_query(f"fold_gap1{h}", gated(h, 1)), gap_psum, "gap")
-                    exp20 = narrow.tile([P, N], BF16, name="exp20")
-                    nc.scalar.activation(exp20[:], gap20[:], EXP, bias=gap_bias[:, 1, h : h + 1])
-                    nc.vector.tensor_add(denom[:, head], exp10[:], exp20[:])
+                    nc.scalar.activation(exp20[:, across], gap20[:], EXP, bias=gap_bias[:, 1, h : h + 1])
                     gap21 = against_genes(blk, fold_of_difference(h), gap_psum, "gap")
-                    tanh21 = narrow.tile([P, N], BF16, name="tanh21")
+                    tanh21 = tanhs.tile([P, N], BF16, name="tanh21")
                     nc.scalar.activation(tanh21[:], gap21[:], TANH, bias=gap_bias[:, 2, h : h + 1], scale=0.5)
-
-                    swing = against_genes(blk, folded_query(f"fold_swing{h}", fixed(h, SWING)), score_psum, "score")
-                    swung = narrow.tile([P, N], BF16, name="swung")
-                    nc.vector.tensor_mul(swung[:], swing[:], tanh21[:])
-                    rise = against_genes(blk, folded_query(f"fold_rise{h}", fixed(h, RISE)), score_psum, "score")
-                    nc.vector.tensor_add(spread[:, head], rise[:], swung[:])
-
-                capped = wide.tile([P, H * N], BF16, name="capped")
+                    tanh_of[blk].append(tanh21)
+                denom = wide.tile([P, H * N], BF16, name="denom")
+                nc.vector.tensor_add(denom[:], exp10[:], exp20[:])
+                capped = cappeds.tile([P, H * N], BF16, name="capped")
                 nc.vector.tensor_scalar(capped[:], denom[:], 1.0, CAP, ADD, MIN)
                 product = narrow.tile([P, N], BF16, name="product")
                 nc.vector.tensor_mul(product[:], capped[:, :N], capped[:, N:])
                 nc.vector.tensor_mul(square, product[:], product[:])
+                capped_of[blk] = capped
+
+            def blend(blk):
+                spread = spreads.tile([P, H * N], BF16, name="spread")
+                for h in range(H):
+                    head = slice(h * N, (h + 1) * N)
+                    swing = against_genes(blk, folded_query(f"fold_swing{h}", fixed(h, SWING)), score_psum, "score")
+                    swung = narrow.tile([P, N], BF16, name="swung")
+                    nc.vector.tensor_mul(swung[:], swing[:], tanh_of[blk][h][:])
+                    rise = against_genes(blk, folded_query(f"fold_rise{h}", fixed(h, RISE)), score_psum, "score")
+                    nc.vector.tensor_add(spread[:, head], rise[:], swung[:])
                 weighted = wide.tile([P, H * N], BF16, name="weighted")
-                nc.vector.tensor_mul(weighted[:, :N], capped[:, N:], spread[:, :N])
-                nc.vector.tensor_mul(weighted[:, N:], capped[:, :N], spread[:, N:])
+                nc.vector.tensor_mul(weighted[:], capped_of[blk][:], spread[:])
                 owed = oweds.tile([P, N], BF16, name="owed")
                 nc.vector.tensor_add(owed[:], weighted[:, :N], weighted[:, N:])
                 spread_of[blk], owed_of[blk] = spread, owed
@@ -213,7 +220,7 @@ def tile_multiheadefralayer_nomp_b_kernel(
                 back = narrow.tile([P, N], BF16, name="back")
                 nc.vector.tensor_mul(back[:], inverse, owed_of[blk][:])
                 fold_first = folded_query("fold_first", fixed(0, FIRST) + fixed(1, FIRST))
-                result = wide.tile([P, N], F32, name="result")
+                result = results.tile([P, N], F32, name="result")
                 for piece in range(PIECES):
                     total = sum_psum.tile([P, PIECE], F32, name="sum")
                     nc.tensor.matmul(total[:], genes(blk), fold_first[:, piece_columns(piece)], start=True, stop=False)
@@ -224,15 +231,20 @@ def tile_multiheadefralayer_nomp_b_kernel(
                     nc.vector.tensor_copy(result[:, piece_columns(piece)], total[:])
                 nc.sync.dma_start(out[blk * P : (blk + 1) * P, :], result[:])
 
-            inverse_before = None
+            inverse_of = {}
             for start in range(0, BLOCKS, BATCH):
                 squares = batches.tile([P, BATCH * N], BF16, name="squares")
                 for i in range(BATCH):
-                    mix(start + i, squares[:, i * N : (i + 1) * N])
-                    if inverse_before is not None:
-                        finish(start - BATCH + i, inverse_before[:, i * N : (i + 1) * N])
+                    blk = start + i
+                    gates(blk, squares[:, i * N : (i + 1) * N])
+                    if blk >= 1:
+                        blend(blk - 1)
+                    if blk >= BATCH:
+                        finish(blk - BATCH, inverse_of[blk - BATCH])
                 inverses = batches.tile([P, BATCH * N], BF16, name="inverses")
                 nc.scalar.activation(inverses[:], squares[:], ROOT)
-                inverse_before = inverses
-            for i in range(BATCH):
-                finish(BLOCKS - BATCH + i, inverse_before[:, i * N : (i + 1) * N])
+                for i in range(BATCH):
+                    inverse_of[start + i] = inverses[:, i * N : (i + 1) * N]
+            blend(BLOCKS - 1)
+            for blk in range(BLOCKS - BATCH, BLOCKS):
+                finish(blk, inverse_of[blk])

@@ -8,6 +8,7 @@ P = 128
 BLOCKS = S // P
 PIECE = 512
 PIECES = N // PIECE
+BANK_BF16 = 1024
 BATCH = 4
 CAP = 2.0 ** 30
 
@@ -19,7 +20,7 @@ EXP = mybir.ActivationFunctionType.Exp
 TANH = mybir.ActivationFunctionType.Tanh
 ROOT = mybir.ActivationFunctionType.Abs_reciprocal_sqrt
 
-GAPS = ((1, 0), (2, 0), (2, 1))
+GAPS = {"gap10": (1, 0), "gap20": (2, 0), "gap21": (2, 1)}
 SWING = {1: -0.5 / H, 2: 0.5 / H}
 RISE = {0: -1.0 / H, 1: 0.5 / H, 2: 0.5 / H}
 FIRST = {0: 1.0 / H}
@@ -27,6 +28,10 @@ FIRST = {0: 1.0 / H}
 
 def piece_columns(piece):
     return slice(piece * PIECE, (piece + 1) * PIECE)
+
+
+def head_columns(h):
+    return slice(h * N, (h + 1) * N)
 
 
 def tile_multiheadefralayer_nomp_b_kernel(
@@ -39,12 +44,15 @@ def tile_multiheadefralayer_nomp_b_kernel(
         tc.tile_pool(name="held", bufs=1) as held,
         tc.tile_pool(name="tanhs", bufs=3 * H) as tanhs,
         tc.tile_pool(name="cappeds", bufs=3) as cappeds,
-        tc.tile_pool(name="results", bufs=4) as results,
-        tc.tile_pool(name="batches", bufs=2) as batches,
         tc.tile_pool(name="spreads", bufs=2 * BATCH) as spreads,
         tc.tile_pool(name="oweds", bufs=2 * BATCH) as oweds,
+        tc.tile_pool(name="batches", bufs=2) as batches,
+        tc.tile_pool(name="results", bufs=BATCH) as results,
         tc.tile_pool(name="narrow", bufs=3) as narrow,
         tc.tile_pool(name="wide", bufs=2) as wide,
+        tc.psum_pool(name="gap_psum", bufs=3) as gap_psum,
+        tc.psum_pool(name="score_psum", bufs=2) as score_psum,
+        tc.psum_pool(name="sum_psum", bufs=3) as sum_psum,
     ):
         identity = held.tile([P, P], BF16, name="identity")
         make_identity(nc, identity[:])
@@ -69,182 +77,183 @@ def tile_multiheadefralayer_nomp_b_kernel(
 
         gate = held.tile([P, H * E * E], F32, name="gate")
         nc.scalar.dma_start(gate[:], gate_w.rearrange("h e f -> (h e f)").partition_broadcast(P))
-        gate_bias = held.tile([P, H * E], F32, name="gate_bias")
-        nc.scalar.dma_start(gate_bias[:], gate_b.rearrange("h f -> (h f)").partition_broadcast(P))
+        gate_shift = held.tile([P, H * E], F32, name="gate_shift")
+        nc.scalar.dma_start(gate_shift[:], gate_b.rearrange("h f -> (h f)").partition_broadcast(P))
 
         gate_by_f = gate[:].rearrange("p (a f) -> p a f", f=E)
-        bias_by_f = gate_bias[:].rearrange("p (h f) -> p h f", f=E)
-        gap_weight = held.tile([P, 2, H * E], F32, name="gap_weight")
-        gap_bias = held.tile([P, len(GAPS), H], F32, name="gap_bias")
-        for g, (high, low) in enumerate(GAPS):
-            if g < 2:
-                nc.vector.tensor_sub(gap_weight[:, g, :], gate_by_f[:, :, high], gate_by_f[:, :, low])
-            nc.vector.tensor_sub(gap_bias[:, g, :], bias_by_f[:, :, high], bias_by_f[:, :, low])
-        nc.vector.tensor_scalar_mul(gap_bias[:, 2, :], gap_bias[:, 2, :], 0.5)
+        shift_by_f = gate_shift[:].rearrange("p (h f) -> p h f", f=E)
+        gap_weight, gap_bias = {}, {}
+        for kind, (high, low) in GAPS.items():
+            if kind != "gap21":
+                gap_weight[kind] = held.tile([P, H * E], F32, name=f"{kind}_weight")
+                nc.vector.tensor_sub(gap_weight[kind][:], gate_by_f[:, :, high], gate_by_f[:, :, low])
+            gap_bias[kind] = held.tile([P, H], F32, name=f"{kind}_bias")
+            nc.vector.tensor_sub(gap_bias[kind][:], shift_by_f[:, :, high], shift_by_f[:, :, low])
+        nc.vector.tensor_scalar_mul(gap_bias["gap21"][:], gap_bias["gap21"][:], 0.5)
 
         table = held.tile([D, S], BF16, name="table")
-        qry = [[held.tile([DK, N], BF16, name=f"qry{e}{h}") for h in range(H)] for e in range(E)]
+        per_bank = BANK_BF16 // P
+        for bank in range(BLOCKS // per_bank):
+            z_flipped = gap_psum.tile([D, BANK_BF16], BF16, name="z_flipped", tag="gap")
+            for i in range(per_bank):
+                nc.tensor.transpose(z_flipped[:, i * P : (i + 1) * P], z_rows[:, bank * per_bank + i, :], identity[:])
+            if bank % 2 == 0:
+                nc.vector.tensor_copy(table[:, bank * BANK_BF16 : (bank + 1) * BANK_BF16], z_flipped[:])
+            else:
+                nc.scalar.copy(table[:, bank * BANK_BF16 : (bank + 1) * BANK_BF16], z_flipped[:])
 
-        with (
-            tc.psum_pool(name="gap_psum", bufs=3) as gap_psum,
-            tc.psum_pool(name="score_psum", bufs=2) as score_psum,
-            tc.psum_pool(name="sum_psum", bufs=3) as sum_psum,
-        ):
-            per_bank = 1024 // P
-            for bank in range(BLOCKS // per_bank):
-                flipped = gap_psum.tile([D, per_bank * P], BF16, name="gap")
-                for i in range(per_bank):
-                    nc.tensor.transpose(flipped[:, i * P : (i + 1) * P], z_rows[:, bank * per_bank + i, :], identity[:])
-                columns = slice(bank * per_bank * P, (bank + 1) * per_bank * P)
-                if bank % 2 == 0:
-                    nc.vector.tensor_copy(table[:, columns], flipped[:])
-                else:
-                    nc.scalar.copy(table[:, columns], flipped[:])
+        def wk_columns(e, h):
+            return slice((e * H + h) * D, (e * H + h + 1) * D)
 
-            wk_flipped = score_psum.tile([DK, E * H * D], BF16, name="score")
-            for e in range(E):
-                for h in range(H):
-                    block = e * H + h
-                    nc.tensor.transpose(wk_flipped[:, block * D : (block + 1) * D], wk[e][:, h * DK : (h + 1) * DK], identity[:])
-            wk_t = held.tile([DK, E * H * D], BF16, name="wk_t")
-            nc.vector.tensor_copy(wk_t[:], wk_flipped[:])
-
-            turn = 0
+        wk_flipped = score_psum.tile([DK, E * H * D], BF16, name="wk_flipped", tag="score")
+        for e in range(E):
             for h in range(H):
-                for e in range(E):
-                    for piece in range(PIECES):
-                        acc = sum_psum.tile([DK, PIECE], F32, name="sum")
-                        looked_up = table[:].indirect(offsets[:, piece * (PIECE // 16) : (piece + 1) * (PIECE // 16)])
-                        nc.tensor.matmul(acc[:], wq[e][:, h * DK : (h + 1) * DK], looked_up, start=True, stop=True)
-                        if turn % 2 == 0:
-                            nc.vector.tensor_copy(qry[e][h][:, piece_columns(piece)], acc[:])
-                        else:
-                            nc.scalar.copy(qry[e][h][:, piece_columns(piece)], acc[:])
-                        turn += 1
+                nc.tensor.transpose(wk_flipped[:, wk_columns(e, h)], wk[e][:, h * DK : (h + 1) * DK], identity[:])
+        wk_t = held.tile([DK, E * H * D], BF16, name="wk_t")
+        nc.vector.tensor_copy(wk_t[:], wk_flipped[:])
 
-            def fold(name, terms):
-                mixers = []
-                for h, e, column, number in terms:
-                    mixer = held.tile([DK, D], BF16, name=f"{name}_mixer{h}{e}")
-                    block = e * H + h
-                    source = wk_t[:, block * D : (block + 1) * D]
-                    if column is None:
-                        nc.vector.tensor_scalar_mul(mixer[:], source, number)
+        qry = [[held.tile([DK, N], BF16, name=f"qry{e}{h}") for h in range(H)] for e in range(E)]
+        turn = 0
+        for h in range(H):
+            for e in range(E):
+                for piece in range(PIECES):
+                    projected = sum_psum.tile([DK, PIECE], F32, name="projected", tag="sum")
+                    looked_up = table[:].indirect(offsets[:, piece * (PIECE // 16) : (piece + 1) * (PIECE // 16)])
+                    nc.tensor.matmul(projected[:], wq[e][:, h * DK : (h + 1) * DK], looked_up, start=True, stop=True)
+                    if turn % 2 == 0:
+                        nc.vector.tensor_copy(qry[e][h][:, piece_columns(piece)], projected[:])
                     else:
-                        nc.vector.tensor_scalar(mixer[:], source, column, number, MULT, MULT)
-                    mixers.append(mixer)
-                folded = held.tile([D, N], BF16, name=name)
-                for piece in range(PIECES):
-                    acc = sum_psum.tile([D, PIECE], F32, name="sum")
-                    for i, (h, e, column, number) in enumerate(terms):
-                        nc.tensor.matmul(
-                            acc[:], mixers[i][:], qry[e][h][:, piece_columns(piece)],
-                            start=(i == 0), stop=(i == len(terms) - 1),
-                        )
-                    nc.vector.tensor_copy(folded[:, piece_columns(piece)], acc[:])
-                return folded
+                        nc.scalar.copy(qry[e][h][:, piece_columns(piece)], projected[:])
+                    turn += 1
 
-            def fixed(h, combination):
-                return [(h, e, None, a * inv_sqrt_dk) for e, a in combination.items()]
-
-            def gated(h, g):
-                return [(h, e, gap_weight[:, g, h * E + e : h * E + e + 1], inv_sqrt_dk) for e in range(E)]
-
-            folds = {}
-
-            def folded_query(name, terms):
-                if name not in folds:
-                    folds[name] = fold(name, terms)
-                return folds[name]
-
-            def fold_of_difference(h):
-                name = f"fold_gap2{h}"
-                if name not in folds:
-                    folds[name] = held.tile([D, N], BF16, name=name)
-                    nc.vector.tensor_sub(folds[name][:], folds[f"fold_gap1{h}"][:], folds[f"fold_gap0{h}"][:])
-                return folds[name]
-
-            spread_of, owed_of, tanh_of, capped_of = {}, {}, {}, {}
-
-            def genes(blk):
-                return table[:, blk * P : (blk + 1) * P]
-
-            def against_genes(blk, folded, pool, tag):
-                product = pool.tile([P, N], BF16, name=tag)
-                for piece in range(PIECES):
+        def fold(name, terms):
+            scaled_keys = []
+            for h, e, column, number in terms:
+                scaled = held.tile([DK, D], BF16, name=f"{name}_keys{h}{e}")
+                if column is None:
+                    nc.vector.tensor_scalar_mul(scaled[:], wk_t[:, wk_columns(e, h)], number)
+                else:
+                    nc.vector.tensor_scalar(scaled[:], wk_t[:, wk_columns(e, h)], column, number, MULT, MULT)
+                scaled_keys.append(scaled)
+            folded = held.tile([D, N], BF16, name=name)
+            for piece in range(PIECES):
+                summed = sum_psum.tile([D, PIECE], F32, name="summed", tag="sum")
+                for i, (h, e, column, number) in enumerate(terms):
                     nc.tensor.matmul(
-                        product[:, piece_columns(piece)], genes(blk), folded[:, piece_columns(piece)],
-                        start=True, stop=True,
+                        summed[:], scaled_keys[i][:], qry[e][h][:, piece_columns(piece)],
+                        start=(i == 0), stop=(i == len(terms) - 1),
                     )
-                return product
+                nc.vector.tensor_copy(folded[:, piece_columns(piece)], summed[:])
+            return folded
 
-            def gates(blk, square):
-                exp10 = wide.tile([P, H * N], BF16, name="exp10")
-                exp20 = wide.tile([P, H * N], BF16, name="exp20")
-                tanh_of[blk] = []
+        def fixed(h, combination):
+            return [(h, e, None, a * inv_sqrt_dk) for e, a in combination.items()]
+
+        def gated(h, kind):
+            return [(h, e, gap_weight[kind][:, h * E + e : h * E + e + 1], inv_sqrt_dk) for e in range(E)]
+
+        folds = {}
+
+        def folded_query(kind, h):
+            name = f"{kind}_fold{h}"
+            if name not in folds:
+                if kind == "gap21":
+                    folds[name] = held.tile([D, N], BF16, name=name)
+                    nc.vector.tensor_sub(folds[name][:], folded_query("gap20", h)[:], folded_query("gap10", h)[:])
+                elif kind == "swing":
+                    folds[name] = fold(name, fixed(h, SWING))
+                elif kind == "rise":
+                    folds[name] = fold(name, fixed(h, RISE))
+                else:
+                    folds[name] = fold(name, gated(h, kind))
+            return folds[name]
+
+        def folded_first():
+            if "first_fold" not in folds:
+                folds["first_fold"] = fold("first_fold", fixed(0, FIRST) + fixed(1, FIRST))
+            return folds["first_fold"]
+
+        tanh_of, capped_of, spread_of, owed_of, inverse_of = {}, {}, {}, {}, {}
+
+        def genes(blk):
+            return table[:, blk * P : (blk + 1) * P]
+
+        def against_genes(blk, folded, pool, name, tag):
+            bank = pool.tile([P, N], BF16, name=name, tag=tag)
+            for piece in range(PIECES):
+                nc.tensor.matmul(
+                    bank[:, piece_columns(piece)], genes(blk), folded[:, piece_columns(piece)], start=True, stop=True
+                )
+            return bank
+
+        def gates(blk, square):
+            denom = wide.tile([P, H * N], BF16, name="denom")
+            tanh_of[blk] = []
+            for h in range(H):
+                gap10 = against_genes(blk, folded_query("gap10", h), gap_psum, "gap10", "gap")
+                exp10 = narrow.tile([P, N], BF16, name="exp10")
+                nc.scalar.activation(exp10[:], gap10[:], EXP, bias=gap_bias["gap10"][:, h : h + 1])
+                gap20 = against_genes(blk, folded_query("gap20", h), gap_psum, "gap20", "gap")
+                exp20 = narrow.tile([P, N], BF16, name="exp20")
+                nc.scalar.activation(exp20[:], gap20[:], EXP, bias=gap_bias["gap20"][:, h : h + 1])
+                nc.vector.tensor_add(denom[:, head_columns(h)], exp10[:], exp20[:])
+                gap21 = against_genes(blk, folded_query("gap21", h), gap_psum, "gap21", "gap")
+                tanh21 = tanhs.tile([P, N], BF16, name="tanh21")
+                nc.scalar.activation(tanh21[:], gap21[:], TANH, bias=gap_bias["gap21"][:, h : h + 1], scale=0.5)
+                tanh_of[blk].append(tanh21)
+            capped = cappeds.tile([P, H * N], BF16, name="capped")
+            nc.vector.tensor_scalar(capped[:], denom[:], 1.0, CAP, ADD, MIN)
+            pair = narrow.tile([P, N], BF16, name="pair")
+            nc.vector.tensor_mul(pair[:], capped[:, head_columns(0)], capped[:, head_columns(1)])
+            nc.vector.tensor_mul(square, pair[:], pair[:])
+            capped_of[blk] = capped
+
+        def blend(blk):
+            spread = spreads.tile([P, H * N], BF16, name="spread")
+            for h in range(H):
+                swing = against_genes(blk, folded_query("swing", h), score_psum, "swing", "score")
+                swung = narrow.tile([P, N], BF16, name="swung")
+                nc.vector.tensor_mul(swung[:], swing[:], tanh_of[blk][h][:])
+                rise = against_genes(blk, folded_query("rise", h), score_psum, "rise", "score")
+                nc.vector.tensor_add(spread[:, head_columns(h)], rise[:], swung[:])
+            weighted = wide.tile([P, H * N], BF16, name="weighted")
+            for h in range(H):
+                nc.vector.tensor_mul(
+                    weighted[:, head_columns(h)], capped_of[blk][:, head_columns(H - 1 - h)], spread[:, head_columns(h)]
+                )
+            owed = oweds.tile([P, N], BF16, name="owed")
+            nc.vector.tensor_add(owed[:], weighted[:, head_columns(0)], weighted[:, head_columns(1)])
+            spread_of[blk], owed_of[blk] = spread, owed
+
+        def finish(blk):
+            back = narrow.tile([P, N], BF16, name="back")
+            nc.vector.tensor_mul(back[:], inverse_of[blk], owed_of[blk][:])
+            result = results.tile([P, N], F32, name="result")
+            for piece in range(PIECES):
+                total = sum_psum.tile([P, PIECE], F32, name="total", tag="sum")
+                nc.tensor.matmul(total[:], genes(blk), folded_first()[:, piece_columns(piece)], start=True, stop=False)
                 for h in range(H):
-                    across = slice((H - 1 - h) * N, (H - h) * N)
-                    gap10 = against_genes(blk, folded_query(f"fold_gap0{h}", gated(h, 0)), gap_psum, "gap")
-                    nc.scalar.activation(exp10[:, across], gap10[:], EXP, bias=gap_bias[:, 0, h : h + 1])
-                    gap20 = against_genes(blk, folded_query(f"fold_gap1{h}", gated(h, 1)), gap_psum, "gap")
-                    nc.scalar.activation(exp20[:, across], gap20[:], EXP, bias=gap_bias[:, 1, h : h + 1])
-                    gap21 = against_genes(blk, fold_of_difference(h), gap_psum, "gap")
-                    tanh21 = tanhs.tile([P, N], BF16, name="tanh21")
-                    nc.scalar.activation(tanh21[:], gap21[:], TANH, bias=gap_bias[:, 2, h : h + 1], scale=0.5)
-                    tanh_of[blk].append(tanh21)
-                denom = wide.tile([P, H * N], BF16, name="denom")
-                nc.vector.tensor_add(denom[:], exp10[:], exp20[:])
-                capped = cappeds.tile([P, H * N], BF16, name="capped")
-                nc.vector.tensor_scalar(capped[:], denom[:], 1.0, CAP, ADD, MIN)
-                product = narrow.tile([P, N], BF16, name="product")
-                nc.vector.tensor_mul(product[:], capped[:, :N], capped[:, N:])
-                nc.vector.tensor_mul(square, product[:], product[:])
-                capped_of[blk] = capped
+                    nc.tensor.matmul(
+                        total[:], identity[:], spread_of[blk][:, h * N + piece * PIECE : h * N + (piece + 1) * PIECE],
+                        start=False, stop=False,
+                    )
+                nc.tensor.matmul(total[:], minus_identity[:], back[:, piece_columns(piece)], start=False, stop=True)
+                nc.vector.tensor_copy(result[:, piece_columns(piece)], total[:])
+            nc.sync.dma_start(out[blk * P : (blk + 1) * P, :], result[:])
 
-            def blend(blk):
-                spread = spreads.tile([P, H * N], BF16, name="spread")
-                for h in range(H):
-                    head = slice(h * N, (h + 1) * N)
-                    swing = against_genes(blk, folded_query(f"fold_swing{h}", fixed(h, SWING)), score_psum, "score")
-                    swung = narrow.tile([P, N], BF16, name="swung")
-                    nc.vector.tensor_mul(swung[:], swing[:], tanh_of[blk][h][:])
-                    rise = against_genes(blk, folded_query(f"fold_rise{h}", fixed(h, RISE)), score_psum, "score")
-                    nc.vector.tensor_add(spread[:, head], rise[:], swung[:])
-                weighted = wide.tile([P, H * N], BF16, name="weighted")
-                nc.vector.tensor_mul(weighted[:], capped_of[blk][:], spread[:])
-                owed = oweds.tile([P, N], BF16, name="owed")
-                nc.vector.tensor_add(owed[:], weighted[:, :N], weighted[:, N:])
-                spread_of[blk], owed_of[blk] = spread, owed
-
-            def finish(blk, inverse):
-                back = narrow.tile([P, N], BF16, name="back")
-                nc.vector.tensor_mul(back[:], inverse, owed_of[blk][:])
-                fold_first = folded_query("fold_first", fixed(0, FIRST) + fixed(1, FIRST))
-                result = results.tile([P, N], F32, name="result")
-                for piece in range(PIECES):
-                    total = sum_psum.tile([P, PIECE], F32, name="sum")
-                    nc.tensor.matmul(total[:], genes(blk), fold_first[:, piece_columns(piece)], start=True, stop=False)
-                    for h in range(H):
-                        columns = slice(h * N + piece * PIECE, h * N + (piece + 1) * PIECE)
-                        nc.tensor.matmul(total[:], identity[:], spread_of[blk][:, columns], start=False, stop=False)
-                    nc.tensor.matmul(total[:], minus_identity[:], back[:, piece_columns(piece)], start=False, stop=True)
-                    nc.vector.tensor_copy(result[:, piece_columns(piece)], total[:])
-                nc.sync.dma_start(out[blk * P : (blk + 1) * P, :], result[:])
-
-            inverse_of = {}
-            for start in range(0, BLOCKS, BATCH):
-                squares = batches.tile([P, BATCH * N], BF16, name="squares")
-                for i in range(BATCH):
-                    blk = start + i
-                    gates(blk, squares[:, i * N : (i + 1) * N])
-                    if blk >= 1:
-                        blend(blk - 1)
-                    if blk >= BATCH:
-                        finish(blk - BATCH, inverse_of[blk - BATCH])
-                inverses = batches.tile([P, BATCH * N], BF16, name="inverses")
-                nc.scalar.activation(inverses[:], squares[:], ROOT)
-                for i in range(BATCH):
-                    inverse_of[start + i] = inverses[:, i * N : (i + 1) * N]
-            blend(BLOCKS - 1)
-            for blk in range(BLOCKS - BATCH, BLOCKS):
-                finish(blk, inverse_of[blk])
+        for first_blk in range(0, BLOCKS, BATCH):
+            squares = batches.tile([P, BATCH * N], BF16, name="squares")
+            for i in range(BATCH):
+                blk = first_blk + i
+                gates(blk, squares[:, i * N : (i + 1) * N])
+                if blk >= 1:
+                    blend(blk - 1)
+                if blk >= BATCH:
+                    finish(blk - BATCH)
+            inverses = batches.tile([P, BATCH * N], BF16, name="inverses")
+            nc.scalar.activation(inverses[:], squares[:], ROOT)
+            for i in range(BATCH):
+                inverse_of[first_blk + i] = inverses[:, i * N : (i + 1) * N]
+        blend(BLOCKS - 1)
+        for blk in range(BLOCKS - BATCH, BLOCKS):
+            finish(blk)

@@ -9,7 +9,9 @@ BLOCKS = S // P
 PIECE = 512
 PIECES = N // PIECE
 BANK_BF16 = 1024
-BATCH = 4
+BATCHES = (5, 5, 5, 1)
+assert sum(BATCHES) == BLOCKS
+LARGEST = max(BATCHES)
 CAP = 2.0 ** 30
 
 FLOPS = 2 * (N + S) * D * H * DK * E + 2 * S * N * DK * H * E
@@ -44,10 +46,10 @@ def tile_multiheadefralayer_nomp_b_kernel(
         tc.tile_pool(name="held", bufs=1) as held,
         tc.tile_pool(name="tanhs", bufs=3 * H) as tanhs,
         tc.tile_pool(name="cappeds", bufs=3) as cappeds,
-        tc.tile_pool(name="spreads", bufs=2 * BATCH) as spreads,
-        tc.tile_pool(name="oweds", bufs=2 * BATCH) as oweds,
+        tc.tile_pool(name="spreads", bufs=LARGEST + 2) as spreads,
+        tc.tile_pool(name="oweds", bufs=LARGEST + 2) as oweds,
         tc.tile_pool(name="batches", bufs=2) as batches,
-        tc.tile_pool(name="results", bufs=BATCH) as results,
+        tc.tile_pool(name="results", bufs=4) as results,
         tc.tile_pool(name="narrow", bufs=3) as narrow,
         tc.tile_pool(name="wide", bufs=2) as wide,
         tc.psum_pool(name="gap_psum", bufs=3) as gap_psum,
@@ -56,8 +58,6 @@ def tile_multiheadefralayer_nomp_b_kernel(
     ):
         identity = held.tile([P, P], BF16, name="identity")
         make_identity(nc, identity[:])
-        minus_identity = held.tile([P, P], BF16, name="minus_identity")
-        nc.gpsimd.tensor_scalar_mul(minus_identity[:], identity[:], -1.0)
 
         offsets = held.tile([P, N // 16], U16, name="offsets")
         nc.sync.dma_start(offsets[:], offs)
@@ -235,25 +235,27 @@ def tile_multiheadefralayer_nomp_b_kernel(
                 for h in range(H):
                     nc.tensor.matmul(
                         total[:], identity[:], spread_of[blk][:, h * N + piece * PIECE : h * N + (piece + 1) * PIECE],
-                        start=False, stop=False,
+                        start=False, stop=(h == H - 1),
                     )
-                nc.tensor.matmul(total[:], minus_identity[:], back[:, piece_columns(piece)], start=False, stop=True)
-                nc.vector.tensor_copy(result[:, piece_columns(piece)], total[:])
+                nc.vector.tensor_sub(result[:, piece_columns(piece)], total[:], back[:, piece_columns(piece)])
             nc.sync.dma_start(out[blk * P : (blk + 1) * P, :], result[:])
 
-        for first_blk in range(0, BLOCKS, BATCH):
-            squares = batches.tile([P, BATCH * N], BF16, name="squares")
-            for i in range(BATCH):
+        first_blk = 0
+        earlier = []
+        for size in BATCHES:
+            squares = batches.tile([P, size * N], BF16, name="squares")
+            for i in range(size):
                 blk = first_blk + i
                 gates(blk, squares[:, i * N : (i + 1) * N])
                 if blk >= 1:
                     blend(blk - 1)
-                if blk >= BATCH:
-                    finish(blk - BATCH)
-            inverses = batches.tile([P, BATCH * N], BF16, name="inverses")
-            nc.scalar.activation(inverses[:], squares[:], ROOT)
-            for i in range(BATCH):
-                inverse_of[first_blk + i] = inverses[:, i * N : (i + 1) * N]
+                for waiting in earlier[i * len(earlier) // size : (i + 1) * len(earlier) // size]:
+                    finish(waiting)
+            nc.scalar.activation(squares[:], squares[:], ROOT)
+            for i in range(size):
+                inverse_of[first_blk + i] = squares[:, i * N : (i + 1) * N]
+            earlier = list(range(first_blk, first_blk + size))
+            first_blk += size
         blend(BLOCKS - 1)
-        for blk in range(BLOCKS - BATCH, BLOCKS):
-            finish(blk)
+        for waiting in earlier:
+            finish(waiting)

@@ -23,9 +23,7 @@ TANH = mybir.ActivationFunctionType.Tanh
 ROOT = mybir.ActivationFunctionType.Abs_reciprocal_sqrt
 
 GAPS = {"gap10": (1, 0), "gap20": (2, 0), "gap21": (2, 1)}
-SWING = {1: -0.5 / H, 2: 0.5 / H}
-RISE = {0: -1.0 / H, 1: 0.5 / H, 2: 0.5 / H}
-FIRST = {0: 1.0 / H}
+PART = {0: 1.0 / H, 1: 0.5 / H, 2: 0.5 / H}
 
 
 def piece_columns(piece):
@@ -66,8 +64,7 @@ def tile_multiheadefralayer_nomp_b_kernel(
         z_blocks = z.rearrange("(b p) c -> p b c", p=P)
         quarter = BLOCKS // 4
         for i in range(4):
-            queue = nc.sync if i % 2 == 0 else nc.scalar
-            queue.dma_start(z_rows[:, i * quarter : (i + 1) * quarter, :], z_blocks[:, i * quarter : (i + 1) * quarter, :])
+            nc.sync.dma_start(z_rows[:, i * quarter : (i + 1) * quarter, :], z_blocks[:, i * quarter : (i + 1) * quarter, :])
 
         wq = [held.tile([D, H * DK], BF16, name=f"wq{e}") for e in range(E)]
         wk = [held.tile([D, H * DK], BF16, name=f"wk{e}") for e in range(E)]
@@ -127,30 +124,30 @@ def tile_multiheadefralayer_nomp_b_kernel(
                     turn += 1
 
         def fold(name, terms):
-            scaled_keys = []
-            for h, e, column, number in terms:
-                scaled = held.tile([DK, D], BF16, name=f"{name}_keys{h}{e}")
-                if column is None:
-                    nc.vector.tensor_scalar_mul(scaled[:], wk_t[:, wk_columns(e, h)], number)
-                else:
-                    nc.vector.tensor_scalar(scaled[:], wk_t[:, wk_columns(e, h)], column, number, MULT, MULT)
-                scaled_keys.append(scaled)
             folded = held.tile([D, N], BF16, name=name)
+            summed = sum_psum.tile([D, N], BF16, name="summed", tag="sum")
             for piece in range(PIECES):
-                summed = sum_psum.tile([D, PIECE], F32, name="summed", tag="sum")
-                for i, (h, e, column, number) in enumerate(terms):
+                for i, (scaled_keys, queries) in enumerate(terms):
                     nc.tensor.matmul(
-                        summed[:], scaled_keys[i][:], qry[e][h][:, piece_columns(piece)],
+                        summed[:, piece_columns(piece)], scaled_keys, queries[:, piece_columns(piece)],
                         start=(i == 0), stop=(i == len(terms) - 1),
                     )
-                nc.vector.tensor_copy(folded[:, piece_columns(piece)], summed[:])
+            nc.vector.tensor_copy(folded[:], summed[:])
             return folded
 
-        def fixed(h, combination):
-            return [(h, e, None, a * inv_sqrt_dk) for e, a in combination.items()]
+        part_keys = held.tile([DK, E * H * D], BF16, name="part_keys")
+        for e in range(E):
+            both_heads = slice(wk_columns(e, 0).start, wk_columns(e, H - 1).stop)
+            nc.vector.tensor_scalar_mul(part_keys[:, both_heads], wk_t[:, both_heads], PART[e] * inv_sqrt_dk)
 
         def gated(h, kind):
-            return [(h, e, gap_weight[kind][:, h * E + e : h * E + e + 1], inv_sqrt_dk) for e in range(E)]
+            terms = []
+            for e in range(E):
+                scaled_keys = held.tile([DK, D], BF16, name=f"{kind}_keys{h}{e}")
+                gate_difference = gap_weight[kind][:, h * E + e : h * E + e + 1]
+                nc.vector.tensor_scalar(scaled_keys[:], wk_t[:, wk_columns(e, h)], gate_difference, inv_sqrt_dk, MULT, MULT)
+                terms.append((scaled_keys[:], qry[e][h]))
+            return terms
 
         folds = {}
 
@@ -161,16 +158,24 @@ def tile_multiheadefralayer_nomp_b_kernel(
                     folds[name] = held.tile([D, N], BF16, name=name)
                     nc.vector.tensor_sub(folds[name][:], folded_query("gap20", h)[:], folded_query("gap10", h)[:])
                 elif kind == "swing":
-                    folds[name] = fold(name, fixed(h, SWING))
+                    folds[name] = held.tile([D, N], BF16, name=name)
+                    nc.vector.tensor_sub(folds[name][:], folded_query("part2", h)[:], folded_query("part1", h)[:])
                 elif kind == "rise":
-                    folds[name] = fold(name, fixed(h, RISE))
+                    middle = held.tile([D, N], BF16, name=f"middle_fold{h}")
+                    nc.vector.tensor_add(middle[:], folded_query("part1", h)[:], folded_query("part2", h)[:])
+                    folds[name] = held.tile([D, N], BF16, name=name)
+                    nc.vector.tensor_sub(folds[name][:], middle[:], folded_query("part0", h)[:])
+                elif kind.startswith("part"):
+                    e = int(kind[-1])
+                    folds[name] = fold(name, [(part_keys[:, wk_columns(e, h)], qry[e][h])])
                 else:
                     folds[name] = fold(name, gated(h, kind))
             return folds[name]
 
         def folded_first():
             if "first_fold" not in folds:
-                folds["first_fold"] = fold("first_fold", fixed(0, FIRST) + fixed(1, FIRST))
+                folds["first_fold"] = held.tile([D, N], BF16, name="first_fold")
+                nc.vector.tensor_add(folds["first_fold"][:], folded_query("part0", 0)[:], folded_query("part0", 1)[:])
             return folds["first_fold"]
 
         tanh_of, capped_of, spread_of, owed_of, inverse_of = {}, {}, {}, {}, {}

@@ -56,6 +56,8 @@ def tile_multiheadefralayer_nomp_b_kernel(
     ):
         identity = held.tile([P, P], BF16, name="identity")
         make_identity(nc, identity[:])
+        minus_identity = held.tile([P, P], BF16, name="minus_identity")
+        nc.gpsimd.tensor_scalar_mul(minus_identity[:], identity[:], -1.0)
 
         offsets = held.tile([P, N // 16], U16, name="offsets")
         nc.sync.dma_start(offsets[:], offs)
@@ -235,14 +237,19 @@ def tile_multiheadefralayer_nomp_b_kernel(
             nc.vector.tensor_mul(back[:], inverse_of[blk], owed_of[blk][:])
             result = results.tile([P, N], F32, name="result")
             for piece in range(PIECES):
+                scalar_copies = blk >= BLOCKS // 2 and piece == PIECES - 1
                 total = sum_psum.tile([P, PIECE], F32, name="total", tag="sum")
                 nc.tensor.matmul(total[:], genes(blk), folded_first()[:, piece_columns(piece)], start=True, stop=False)
                 for h in range(H):
                     nc.tensor.matmul(
                         total[:], identity[:], spread_of[blk][:, h * N + piece * PIECE : h * N + (piece + 1) * PIECE],
-                        start=False, stop=(h == H - 1),
+                        start=False, stop=(h == H - 1 and not scalar_copies),
                     )
-                nc.vector.tensor_sub(result[:, piece_columns(piece)], total[:], back[:, piece_columns(piece)])
+                if scalar_copies:
+                    nc.tensor.matmul(total[:], minus_identity[:], back[:, piece_columns(piece)], start=False, stop=True)
+                    nc.scalar.copy(result[:, piece_columns(piece)], total[:])
+                else:
+                    nc.vector.tensor_sub(result[:, piece_columns(piece)], total[:], back[:, piece_columns(piece)])
             nc.sync.dma_start(out[blk * P : (blk + 1) * P, :], result[:])
 
         first_blk = 0

@@ -237,7 +237,7 @@ def tile_multiheadefralayer_nomp_b_kernel(
             nc.vector.tensor_mul(back[:], inverse_of[blk], owed_of[blk][:])
             result = results.tile([P, N], F32, name="result")
             for piece in range(PIECES):
-                scalar_copies = blk >= BLOCKS // 2 and piece == PIECES - 1
+                scalar_copies = blk >= sum(BATCHES[:-2]) and piece == PIECES - 1
                 total = sum_psum.tile([P, PIECE], F32, name="total", tag="sum")
                 nc.tensor.matmul(total[:], genes(blk), folded_first()[:, piece_columns(piece)], start=True, stop=False)
                 for h in range(H):

@@ -9,21 +9,19 @@ BLOCKS = S // P
 PIECE = 512
 PIECES = N // PIECE
 BANK_BF16 = 1024
-BATCHES = (5, 5, 5, 1)
+BATCHES = (4, 4, 4, 4)
 assert sum(BATCHES) == BLOCKS
 LARGEST = max(BATCHES)
-CAP = 2.0 ** 30
+FLOOR = 2.0 ** -64
 
 FLOPS = 2 * (N + S) * D * H * DK * E + 2 * S * N * DK * H * E
 
 BF16, F32, U16 = mybir.dt.bfloat16, mybir.dt.float32, mybir.dt.uint16
-MULT, ADD, MIN = mybir.AluOpType.mult, mybir.AluOpType.add, mybir.AluOpType.min
-EXP = mybir.ActivationFunctionType.Exp
-TANH = mybir.ActivationFunctionType.Tanh
-ROOT = mybir.ActivationFunctionType.Abs_reciprocal_sqrt
+MULT, MIN = mybir.AluOpType.mult, mybir.AluOpType.min
+SIGMOID = mybir.ActivationFunctionType.Sigmoid
+LN = mybir.ActivationFunctionType.Ln
 
-GAPS = {"gap10": (1, 0), "gap20": (2, 0), "gap21": (2, 1)}
-PART = {0: 1.0 / H, 1: 0.5 / H, 2: 0.5 / H}
+GAPS = {"gap21": (2, 1), "gap20": (2, 0)}
 
 
 def piece_columns(piece):
@@ -42,22 +40,19 @@ def tile_multiheadefralayer_nomp_b_kernel(
 
     with (
         tc.tile_pool(name="held", bufs=1) as held,
-        tc.tile_pool(name="tanhs", bufs=3 * H) as tanhs,
-        tc.tile_pool(name="cappeds", bufs=3) as cappeds,
-        tc.tile_pool(name="spreads", bufs=LARGEST + 2) as spreads,
-        tc.tile_pool(name="oweds", bufs=LARGEST + 2) as oweds,
-        tc.tile_pool(name="batches", bufs=2) as batches,
-        tc.tile_pool(name="results", bufs=4) as results,
+        tc.tile_pool(name="kept_gaps", bufs=LARGEST + 1) as kept_gaps,
+        tc.tile_pool(name="shares", bufs=LARGEST + 1) as shares,
+        tc.tile_pool(name="mixes", bufs=LARGEST + 1) as mixes,
+        tc.tile_pool(name="leads", bufs=LARGEST + 1) as leads,
+        tc.tile_pool(name="wide", bufs=3) as wide,
         tc.tile_pool(name="narrow", bufs=3) as narrow,
-        tc.tile_pool(name="wide", bufs=2) as wide,
+        tc.tile_pool(name="results", bufs=4) as results,
         tc.psum_pool(name="gap_psum", bufs=3) as gap_psum,
         tc.psum_pool(name="score_psum", bufs=2) as score_psum,
         tc.psum_pool(name="sum_psum", bufs=3) as sum_psum,
     ):
         identity = held.tile([P, P], BF16, name="identity")
         make_identity(nc, identity[:])
-        minus_identity = held.tile([P, P], BF16, name="minus_identity")
-        nc.gpsimd.tensor_scalar_mul(minus_identity[:], identity[:], -1.0)
 
         offsets = held.tile([P, N // 16], U16, name="offsets")
         nc.sync.dma_start(offsets[:], offs)
@@ -79,16 +74,17 @@ def tile_multiheadefralayer_nomp_b_kernel(
         gate_shift = held.tile([P, H * E], F32, name="gate_shift")
         nc.scalar.dma_start(gate_shift[:], gate_b.rearrange("h f -> (h f)").partition_broadcast(P))
 
+        floor = held.tile([P, 1], F32, name="floor")
+        nc.vector.memset(floor[:], FLOOR)
+
         gate_by_f = gate[:].rearrange("p (a f) -> p a f", f=E)
         shift_by_f = gate_shift[:].rearrange("p (h f) -> p h f", f=E)
         gap_weight, gap_bias = {}, {}
         for kind, (high, low) in GAPS.items():
-            if kind != "gap21":
-                gap_weight[kind] = held.tile([P, H * E], F32, name=f"{kind}_weight")
-                nc.vector.tensor_sub(gap_weight[kind][:], gate_by_f[:, :, high], gate_by_f[:, :, low])
+            gap_weight[kind] = held.tile([P, H * E], F32, name=f"{kind}_weight")
+            nc.vector.tensor_sub(gap_weight[kind][:], gate_by_f[:, :, high], gate_by_f[:, :, low])
             gap_bias[kind] = held.tile([P, H], F32, name=f"{kind}_bias")
             nc.vector.tensor_sub(gap_bias[kind][:], shift_by_f[:, :, high], shift_by_f[:, :, low])
-        nc.vector.tensor_scalar_mul(gap_bias["gap21"][:], gap_bias["gap21"][:], 0.5)
 
         table = held.tile([D, S], BF16, name="table")
         per_bank = BANK_BF16 // P
@@ -138,9 +134,7 @@ def tile_multiheadefralayer_nomp_b_kernel(
             return folded
 
         part_keys = held.tile([DK, E * H * D], BF16, name="part_keys")
-        for e in range(E):
-            both_heads = slice(wk_columns(e, 0).start, wk_columns(e, H - 1).stop)
-            nc.vector.tensor_scalar_mul(part_keys[:, both_heads], wk_t[:, both_heads], PART[e] * inv_sqrt_dk)
+        nc.vector.tensor_scalar_mul(part_keys[:], wk_t[:], inv_sqrt_dk / H)
 
         def gated(h, kind):
             terms = []
@@ -156,17 +150,12 @@ def tile_multiheadefralayer_nomp_b_kernel(
         def folded_query(kind, h):
             name = f"{kind}_fold{h}"
             if name not in folds:
-                if kind == "gap21":
+                if kind == "step1":
                     folds[name] = held.tile([D, N], BF16, name=name)
-                    nc.vector.tensor_sub(folds[name][:], folded_query("gap20", h)[:], folded_query("gap10", h)[:])
-                elif kind == "swing":
+                    nc.vector.tensor_sub(folds[name][:], folded_query("part1", h)[:], folded_query("part0", h)[:])
+                elif kind == "step2":
                     folds[name] = held.tile([D, N], BF16, name=name)
                     nc.vector.tensor_sub(folds[name][:], folded_query("part2", h)[:], folded_query("part1", h)[:])
-                elif kind == "rise":
-                    middle = held.tile([D, N], BF16, name=f"middle_fold{h}")
-                    nc.vector.tensor_add(middle[:], folded_query("part1", h)[:], folded_query("part2", h)[:])
-                    folds[name] = held.tile([D, N], BF16, name=name)
-                    nc.vector.tensor_sub(folds[name][:], middle[:], folded_query("part0", h)[:])
                 elif kind.startswith("part"):
                     e = int(kind[-1])
                     folds[name] = fold(name, [(part_keys[:, wk_columns(e, h)], qry[e][h])])
@@ -180,7 +169,7 @@ def tile_multiheadefralayer_nomp_b_kernel(
                 nc.vector.tensor_add(folds["first_fold"][:], folded_query("part0", 0)[:], folded_query("part0", 1)[:])
             return folds["first_fold"]
 
-        tanh_of, capped_of, spread_of, owed_of, inverse_of = {}, {}, {}, {}, {}
+        gap21_of, share2_of, mix_of, lead_of, both_of, gain_of, totals_of = {}, {}, {}, {}, {}, {}, {}
 
         def genes(blk):
             return table[:, blk * P : (blk + 1) * P]
@@ -193,81 +182,97 @@ def tile_multiheadefralayer_nomp_b_kernel(
                 )
             return bank
 
-        def gates(blk, square):
-            denom = wide.tile([P, H * N], BF16, name="denom")
-            tanh_of[blk] = []
+        def keep_gap21(blk):
+            gap21_of[blk] = kept_gaps.tile([P, H * N], BF16, name="gap21_kept")
             for h in range(H):
-                gap10 = against_genes(blk, folded_query("gap10", h), gap_psum, "gap10", "gap")
-                exp10 = narrow.tile([P, N], BF16, name="exp10")
-                nc.scalar.activation(exp10[:], gap10[:], EXP, bias=gap_bias["gap10"][:, h : h + 1])
-                gap20 = against_genes(blk, folded_query("gap20", h), gap_psum, "gap20", "gap")
-                exp20 = narrow.tile([P, N], BF16, name="exp20")
-                nc.scalar.activation(exp20[:], gap20[:], EXP, bias=gap_bias["gap20"][:, h : h + 1])
-                nc.vector.tensor_add(denom[:, head_columns(h)], exp10[:], exp20[:])
                 gap21 = against_genes(blk, folded_query("gap21", h), gap_psum, "gap21", "gap")
-                tanh21 = tanhs.tile([P, N], BF16, name="tanh21")
-                nc.scalar.activation(tanh21[:], gap21[:], TANH, bias=gap_bias["gap21"][:, h : h + 1], scale=0.5)
-                tanh_of[blk].append(tanh21)
-            capped = cappeds.tile([P, H * N], BF16, name="capped")
-            nc.vector.tensor_scalar(capped[:], denom[:], 1.0, CAP, ADD, MIN)
-            pair = narrow.tile([P, N], BF16, name="pair")
-            nc.vector.tensor_mul(pair[:], capped[:, head_columns(0)], capped[:, head_columns(1)])
-            nc.vector.tensor_mul(square, pair[:], pair[:])
-            capped_of[blk] = capped
+                nc.vector.tensor_scalar_add(gap21_of[blk][:, head_columns(h)], gap21[:], gap_bias["gap21"][:, h : h + 1])
 
-        def blend(blk):
-            spread = spreads.tile([P, H * N], BF16, name="spread")
+        def first_sigmoid(blk):
+            share2_of[blk] = shares.tile([P, H * N], BF16, name="share2")
             for h in range(H):
-                swing = against_genes(blk, folded_query("swing", h), score_psum, "swing", "score")
-                swung = narrow.tile([P, N], BF16, name="swung")
-                nc.vector.tensor_mul(swung[:], swing[:], tanh_of[blk][h][:])
-                rise = against_genes(blk, folded_query("rise", h), score_psum, "rise", "score")
-                nc.vector.tensor_add(spread[:, head_columns(h)], rise[:], swung[:])
-            weighted = wide.tile([P, H * N], BF16, name="weighted")
+                nc.scalar.activation(share2_of[blk][:, head_columns(h)], gap21_of[blk][:, head_columns(h)], SIGMOID)
+
+        def mix_scores(blk):
+            mix_of[blk] = mixes.tile([P, H * N], BF16, name="mix")
             for h in range(H):
-                nc.vector.tensor_mul(
-                    weighted[:, head_columns(h)], capped_of[blk][:, head_columns(H - 1 - h)], spread[:, head_columns(h)]
+                step2 = against_genes(blk, folded_query("step2", h), score_psum, "step2", "score")
+                shared = narrow.tile([P, N], BF16, name="shared")
+                nc.vector.tensor_mul(shared[:], step2[:], share2_of[blk][:, head_columns(h)])
+                step1 = against_genes(blk, folded_query("step1", h), score_psum, "step1", "score")
+                nc.vector.tensor_add(mix_of[blk][:, head_columns(h)], step1[:], shared[:])
+
+        def logarithm(blk):
+            nc.scalar.activation(share2_of[blk][:], share2_of[blk][:], LN, bias=floor[:, 0:1])
+
+        def find_lead(blk):
+            lead_of[blk] = leads.tile([P, H * N], BF16, name="lead")
+            for h in range(H):
+                log_share = narrow.tile([P, N], BF16, name="log_share")
+                nc.vector.tensor_tensor(log_share[:], share2_of[blk][:, head_columns(h)], gap21_of[blk][:, head_columns(h)], MIN)
+                gap20 = against_genes(blk, folded_query("gap20", h), gap_psum, "gap20", "gap")
+                nc.vector.tensor_sub(lead_of[blk][:, head_columns(h)], gap20[:], log_share[:])
+
+        def second_sigmoid(blk):
+            both_of[blk] = wide.tile([P, H * N], BF16, name="both")
+            for h in range(H):
+                nc.scalar.activation(
+                    both_of[blk][:, head_columns(h)], lead_of[blk][:, head_columns(h)], SIGMOID, bias=gap_bias["gap20"][:, h : h + 1]
                 )
-            owed = oweds.tile([P, N], BF16, name="owed")
-            nc.vector.tensor_add(owed[:], weighted[:, head_columns(0)], weighted[:, head_columns(1)])
-            spread_of[blk], owed_of[blk] = spread, owed
 
-        def finish(blk):
-            back = narrow.tile([P, N], BF16, name="back")
-            nc.vector.tensor_mul(back[:], inverse_of[blk], owed_of[blk][:])
-            result = results.tile([P, N], F32, name="result")
+        def find_gain(blk):
+            gain_of[blk] = wide.tile([P, H * N], BF16, name="gain")
+            nc.vector.tensor_mul(gain_of[blk][:], both_of[blk][:], mix_of[blk][:])
+
+        def sum_up(blk):
+            totals_of[blk] = []
             for piece in range(PIECES):
-                scalar_copies = blk >= sum(BATCHES[:-2]) and piece == PIECES - 1
                 total = sum_psum.tile([P, PIECE], F32, name="total", tag="sum")
                 nc.tensor.matmul(total[:], genes(blk), folded_first()[:, piece_columns(piece)], start=True, stop=False)
                 for h in range(H):
                     nc.tensor.matmul(
-                        total[:], identity[:], spread_of[blk][:, h * N + piece * PIECE : h * N + (piece + 1) * PIECE],
-                        start=False, stop=(h == H - 1 and not scalar_copies),
+                        total[:], identity[:], gain_of[blk][:, h * N + piece * PIECE : h * N + (piece + 1) * PIECE],
+                        start=False, stop=(h == H - 1),
                     )
-                if scalar_copies:
-                    nc.tensor.matmul(total[:], minus_identity[:], back[:, piece_columns(piece)], start=False, stop=True)
-                    nc.scalar.copy(result[:, piece_columns(piece)], total[:])
-                else:
-                    nc.vector.tensor_sub(result[:, piece_columns(piece)], total[:], back[:, piece_columns(piece)])
+                totals_of[blk].append(total)
+
+        def store(blk):
+            result = results.tile([P, N], F32, name="result")
+            for piece in range(PIECES):
+                nc.vector.tensor_copy(result[:, piece_columns(piece)], totals_of[blk][piece][:])
             nc.sync.dma_start(out[blk * P : (blk + 1) * P, :], result[:])
 
-        first_blk = 0
-        earlier = []
+        batches = []
         for size in BATCHES:
-            squares = batches.tile([P, size * N], BF16, name="squares")
-            for i in range(size):
-                blk = first_blk + i
-                gates(blk, squares[:, i * N : (i + 1) * N])
-                if blk >= 1:
-                    blend(blk - 1)
-                for waiting in earlier[i * len(earlier) // size : (i + 1) * len(earlier) // size]:
-                    finish(waiting)
-            nc.scalar.activation(squares[:], squares[:], ROOT)
-            for i in range(size):
-                inverse_of[first_blk + i] = squares[:, i * N : (i + 1) * N]
-            earlier = list(range(first_blk, first_blk + size))
-            first_blk += size
-        blend(BLOCKS - 1)
-        for waiting in earlier:
-            finish(waiting)
+            start = sum(len(batch) for batch in batches)
+            batches.append(list(range(start, start + size)))
+
+        for blk in batches[0]:
+            keep_gap21(blk)
+            first_sigmoid(blk)
+        for blk in batches[0]:
+            mix_scores(blk)
+
+        for k, batch in enumerate(batches):
+            following = batches[k + 1] if k + 1 < len(batches) else []
+            for blk in batch:
+                logarithm(blk)
+            for blk in batch:
+                find_lead(blk)
+            for blk in following:
+                keep_gap21(blk)
+            for i in range(max(len(batch), len(following))):
+                if i < len(batch):
+                    second_sigmoid(batch[i])
+                if i < len(following):
+                    first_sigmoid(following[i])
+                if i < len(batch):
+                    find_gain(batch[i])
+                if i < len(following):
+                    mix_scores(following[i])
+                if 1 <= i <= len(batch):
+                    store(batch[i - 1])
+                if i < len(batch):
+                    sum_up(batch[i])
+            if len(batch) >= len(following):
+                store(batch[-1])

@@ -42,6 +42,7 @@ def tile_multiheadefralayer_nomp_b_kernel(
         tc.tile_pool(name="held", bufs=1) as held,
         tc.tile_pool(name="kept_gaps", bufs=LARGEST + 1) as kept_gaps,
         tc.tile_pool(name="shares", bufs=LARGEST + 1) as shares,
+        tc.tile_pool(name="logs", bufs=LARGEST + 1) as logs,
         tc.tile_pool(name="mixes", bufs=LARGEST + 1) as mixes,
         tc.tile_pool(name="leads", bufs=LARGEST + 1) as leads,
         tc.tile_pool(name="wide", bufs=3) as wide,
@@ -169,7 +170,7 @@ def tile_multiheadefralayer_nomp_b_kernel(
                 nc.vector.tensor_add(folds["first_fold"][:], folded_query("part0", 0)[:], folded_query("part0", 1)[:])
             return folds["first_fold"]
 
-        gap21_of, share2_of, mix_of, lead_of, both_of, gain_of, totals_of = {}, {}, {}, {}, {}, {}, {}
+        gap21_of, share2_of, mix_of, log_of, lead_of, both_of, gain_of, totals_of = {}, {}, {}, {}, {}, {}, {}, {}
 
         def genes(blk):
             return table[:, blk * P : (blk + 1) * P]
@@ -203,13 +204,14 @@ def tile_multiheadefralayer_nomp_b_kernel(
                 nc.vector.tensor_add(mix_of[blk][:, head_columns(h)], step1[:], shared[:])
 
         def logarithm(blk):
-            nc.scalar.activation(share2_of[blk][:], share2_of[blk][:], LN, bias=floor[:, 0:1])
+            log_of[blk] = logs.tile([P, H * N], BF16, name="log_floored")
+            nc.scalar.activation(log_of[blk][:], share2_of[blk][:], LN, bias=floor[:, 0:1])
 
         def find_lead(blk):
             lead_of[blk] = leads.tile([P, H * N], BF16, name="lead")
             for h in range(H):
                 log_share = narrow.tile([P, N], BF16, name="log_share")
-                nc.vector.tensor_tensor(log_share[:], share2_of[blk][:, head_columns(h)], gap21_of[blk][:, head_columns(h)], MIN)
+                nc.vector.tensor_tensor(log_share[:], log_of[blk][:, head_columns(h)], gap21_of[blk][:, head_columns(h)], MIN)
                 gap20 = against_genes(blk, folded_query("gap20", h), gap_psum, "gap20", "gap")
                 nc.vector.tensor_sub(lead_of[blk][:, head_columns(h)], gap20[:], log_share[:])
 
@@ -239,7 +241,10 @@ def tile_multiheadefralayer_nomp_b_kernel(
         def store(blk):
             result = results.tile([P, N], F32, name="result")
             for piece in range(PIECES):
-                nc.vector.tensor_copy(result[:, piece_columns(piece)], totals_of[blk][piece][:])
+                if piece == 1 and blk % 2 == 1:
+                    nc.scalar.copy(result[:, piece_columns(piece)], totals_of[blk][piece][:])
+                else:
+                    nc.vector.tensor_copy(result[:, piece_columns(piece)], totals_of[blk][piece][:])
             nc.sync.dma_start(out[blk * P : (blk + 1) * P, :], result[:])
 
         batches = []

@@ -9,7 +9,7 @@ BLOCKS = S // P
 PIECE = 512
 PIECES = N // PIECE
 BANK_BF16 = 1024
-BATCHES = (4, 4, 4, 4)
+BATCHES = (5, 6, 5)
 assert sum(BATCHES) == BLOCKS
 LARGEST = max(BATCHES)
 FLOOR = 2.0 ** -64
@@ -42,18 +42,20 @@ def tile_multiheadefralayer_nomp_b_kernel(
         tc.tile_pool(name="held", bufs=1) as held,
         tc.tile_pool(name="kept_gaps", bufs=LARGEST + 1) as kept_gaps,
         tc.tile_pool(name="shares", bufs=LARGEST + 1) as shares,
-        tc.tile_pool(name="logs", bufs=LARGEST + 1) as logs,
         tc.tile_pool(name="mixes", bufs=LARGEST + 1) as mixes,
-        tc.tile_pool(name="leads", bufs=LARGEST + 1) as leads,
+        tc.tile_pool(name="leads", bufs=1) as leads,
         tc.tile_pool(name="wide", bufs=3) as wide,
         tc.tile_pool(name="narrow", bufs=3) as narrow,
         tc.tile_pool(name="results", bufs=4) as results,
-        tc.psum_pool(name="gap_psum", bufs=3) as gap_psum,
+        tc.psum_pool(name="gap_psum", bufs=2) as gap_psum,
+        tc.psum_pool(name="lead_psum", bufs=1) as lead_psum,
         tc.psum_pool(name="score_psum", bufs=2) as score_psum,
         tc.psum_pool(name="sum_psum", bufs=3) as sum_psum,
     ):
         identity = held.tile([P, P], BF16, name="identity")
         make_identity(nc, identity[:])
+        minus_identity = held.tile([P, P], BF16, name="minus_identity")
+        nc.gpsimd.tensor_scalar_mul(minus_identity[:], identity[:], -1.0)
 
         offsets = held.tile([P, N // 16], U16, name="offsets")
         nc.sync.dma_start(offsets[:], offs)
@@ -170,7 +172,7 @@ def tile_multiheadefralayer_nomp_b_kernel(
                 nc.vector.tensor_add(folds["first_fold"][:], folded_query("part0", 0)[:], folded_query("part0", 1)[:])
             return folds["first_fold"]
 
-        gap21_of, share2_of, mix_of, log_of, lead_of, both_of, gain_of, totals_of = {}, {}, {}, {}, {}, {}, {}, {}
+        gap21_of, share2_of, mix_of, lead_of, both_of, gain_of, totals_of = {}, {}, {}, {}, {}, {}, {}
 
         def genes(blk):
             return table[:, blk * P : (blk + 1) * P]
@@ -204,23 +206,39 @@ def tile_multiheadefralayer_nomp_b_kernel(
                 nc.vector.tensor_add(mix_of[blk][:, head_columns(h)], step1[:], shared[:])
 
         def logarithm(blk):
-            log_of[blk] = logs.tile([P, H * N], BF16, name="log_floored")
-            nc.scalar.activation(log_of[blk][:], share2_of[blk][:], LN, bias=floor[:, 0:1])
+            nc.scalar.activation(lead_of[blk], share2_of[blk][:], LN, bias=floor[:, 0:1])
+
+        def tensor_subtracts(blk, h):
+            return h == 0 and blk % 2 == 1
 
         def find_lead(blk):
-            lead_of[blk] = leads.tile([P, H * N], BF16, name="lead")
             for h in range(H):
+                if tensor_subtracts(blk, h):
+                    nc.vector.tensor_tensor(
+                        lead_of[blk][:, head_columns(h)], lead_of[blk][:, head_columns(h)], gap21_of[blk][:, head_columns(h)], MIN
+                    )
+                    continue
                 log_share = narrow.tile([P, N], BF16, name="log_share")
-                nc.vector.tensor_tensor(log_share[:], log_of[blk][:, head_columns(h)], gap21_of[blk][:, head_columns(h)], MIN)
+                nc.vector.tensor_tensor(log_share[:], lead_of[blk][:, head_columns(h)], gap21_of[blk][:, head_columns(h)], MIN)
                 gap20 = against_genes(blk, folded_query("gap20", h), gap_psum, "gap20", "gap")
                 nc.vector.tensor_sub(lead_of[blk][:, head_columns(h)], gap20[:], log_share[:])
 
         def second_sigmoid(blk):
             both_of[blk] = wide.tile([P, H * N], BF16, name="both")
             for h in range(H):
-                nc.scalar.activation(
-                    both_of[blk][:, head_columns(h)], lead_of[blk][:, head_columns(h)], SIGMOID, bias=gap_bias["gap20"][:, h : h + 1]
-                )
+                lead = lead_of[blk][:, head_columns(h)]
+                if tensor_subtracts(blk, h):
+                    lead_bank = lead_psum.tile([P, N], BF16, name="lead_bank")
+                    for piece in range(PIECES):
+                        nc.tensor.matmul(
+                            lead_bank[:, piece_columns(piece)], genes(blk), folded_query("gap20", h)[:, piece_columns(piece)],
+                            start=True, stop=False,
+                        )
+                        nc.tensor.matmul(
+                            lead_bank[:, piece_columns(piece)], minus_identity[:], lead[:, piece_columns(piece)], start=False, stop=True
+                        )
+                    lead = lead_bank[:]
+                nc.scalar.activation(both_of[blk][:, head_columns(h)], lead, SIGMOID, bias=gap_bias["gap20"][:, h : h + 1])
 
         def find_gain(blk):
             gain_of[blk] = wide.tile([P, H * N], BF16, name="gain")
@@ -260,7 +278,10 @@ def tile_multiheadefralayer_nomp_b_kernel(
 
         for k, batch in enumerate(batches):
             following = batches[k + 1] if k + 1 < len(batches) else []
-            for blk in batch:
+            leads_of_batch = leads.tile([P, len(batch) * H * N], BF16, name="leads_of_batch")
+            for i, blk in enumerate(batch):
+                lead_of[blk] = leads_of_batch[:, i * H * N : (i + 1) * H * N]
+            for blk in batch[-1:] + batch[:-1]:
                 logarithm(blk)
             for blk in batch:
                 find_lead(blk)

@@ -47,10 +47,10 @@ def tile_multiheadefralayer_nomp_b_kernel(
         tc.tile_pool(name="wide", bufs=3) as wide,
         tc.tile_pool(name="narrow", bufs=3) as narrow,
         tc.tile_pool(name="results", bufs=4) as results,
-        tc.psum_pool(name="gap_psum", bufs=2) as gap_psum,
+        tc.psum_pool(name="gap_psum", bufs=3) as gap_psum,
         tc.psum_pool(name="lead_psum", bufs=1) as lead_psum,
         tc.psum_pool(name="score_psum", bufs=2) as score_psum,
-        tc.psum_pool(name="sum_psum", bufs=3) as sum_psum,
+        tc.psum_pool(name="sum_psum", bufs=2) as sum_psum,
     ):
         identity = held.tile([P, P], BF16, name="identity")
         make_identity(nc, identity[:])
@@ -115,7 +115,10 @@ def tile_multiheadefralayer_nomp_b_kernel(
         for h in range(H):
             for e in range(E):
                 for piece in range(PIECES):
-                    projected = sum_psum.tile([DK, PIECE], F32, name="projected", tag="sum")
+                    if turn % 2 == 0:
+                        projected = sum_psum.tile([DK, PIECE], F32, name="projected", tag="sum")
+                    else:
+                        projected = gap_psum.tile([DK, PIECE], F32, name="projected", tag="gap")
                     looked_up = table[:].indirect(offsets[:, piece * (PIECE // 16) : (piece + 1) * (PIECE // 16)])
                     nc.tensor.matmul(projected[:], wq[e][:, h * DK : (h + 1) * DK], looked_up, start=True, stop=True)
                     if turn % 2 == 0:
@@ -245,24 +248,23 @@ def tile_multiheadefralayer_nomp_b_kernel(
             nc.vector.tensor_mul(gain_of[blk][:], both_of[blk][:], mix_of[blk][:])
 
         def sum_up(blk):
-            totals_of[blk] = []
+            totals_of[blk] = sum_psum.tile([P, N], BF16, name="total", tag="sum")
             for piece in range(PIECES):
-                total = sum_psum.tile([P, PIECE], F32, name="total", tag="sum")
-                nc.tensor.matmul(total[:], genes(blk), folded_first()[:, piece_columns(piece)], start=True, stop=False)
+                total = totals_of[blk][:, piece_columns(piece)]
+                nc.tensor.matmul(total, genes(blk), folded_first()[:, piece_columns(piece)], start=True, stop=False)
                 for h in range(H):
                     nc.tensor.matmul(
-                        total[:], identity[:], gain_of[blk][:, h * N + piece * PIECE : h * N + (piece + 1) * PIECE],
+                        total, identity[:], gain_of[blk][:, h * N + piece * PIECE : h * N + (piece + 1) * PIECE],
                         start=False, stop=(h == H - 1),
                     )
-                totals_of[blk].append(total)
 
         def store(blk):
             result = results.tile([P, N], F32, name="result")
             for piece in range(PIECES):
                 if piece == 1 and blk % 2 == 1:
-                    nc.scalar.copy(result[:, piece_columns(piece)], totals_of[blk][piece][:])
+                    nc.scalar.copy(result[:, piece_columns(piece)], totals_of[blk][:, piece_columns(piece)])
                 else:
-                    nc.vector.tensor_copy(result[:, piece_columns(piece)], totals_of[blk][piece][:])
+                    nc.vector.tensor_copy(result[:, piece_columns(piece)], totals_of[blk][:, piece_columns(piece)])
             nc.sync.dma_start(out[blk * P : (blk + 1) * P, :], result[:])
 
         batches = []

@@ -48,14 +48,11 @@ def tile_multiheadefralayer_nomp_b_kernel(
         tc.tile_pool(name="narrow", bufs=3) as narrow,
         tc.tile_pool(name="results", bufs=4) as results,
         tc.psum_pool(name="gap_psum", bufs=3) as gap_psum,
-        tc.psum_pool(name="lead_psum", bufs=1) as lead_psum,
         tc.psum_pool(name="score_psum", bufs=2) as score_psum,
-        tc.psum_pool(name="sum_psum", bufs=2) as sum_psum,
+        tc.psum_pool(name="sum_psum", bufs=3) as sum_psum,
     ):
         identity = held.tile([P, P], BF16, name="identity")
         make_identity(nc, identity[:])
-        minus_identity = held.tile([P, P], BF16, name="minus_identity")
-        nc.gpsimd.tensor_scalar_mul(minus_identity[:], identity[:], -1.0)
 
         offsets = held.tile([P, N // 16], U16, name="offsets")
         nc.sync.dma_start(offsets[:], offs)
@@ -175,7 +172,7 @@ def tile_multiheadefralayer_nomp_b_kernel(
                 nc.vector.tensor_add(folds["first_fold"][:], folded_query("part0", 0)[:], folded_query("part0", 1)[:])
             return folds["first_fold"]
 
-        gap21_of, share2_of, mix_of, lead_of, both_of, gain_of, totals_of = {}, {}, {}, {}, {}, {}, {}
+        gap21_of, share2_of, shared_of, mix_of, lead_of, both_of, gain_of, totals_of = {}, {}, {}, {}, {}, {}, {}, {}
 
         def genes(blk):
             return table[:, blk * P : (blk + 1) * P]
@@ -199,28 +196,41 @@ def tile_multiheadefralayer_nomp_b_kernel(
             for h in range(H):
                 nc.scalar.activation(share2_of[blk][:, head_columns(h)], gap21_of[blk][:, head_columns(h)], SIGMOID)
 
+        def tensor_mixes(h):
+            return h == 0
+
         def mix_scores(blk):
-            mix_of[blk] = mixes.tile([P, H * N], BF16, name="mix")
             for h in range(H):
                 step2 = against_genes(blk, folded_query("step2", h), score_psum, "step2", "score")
+                if tensor_mixes(h):
+                    shared_of[blk, h] = mixes.tile([P, N], BF16, name="shared_kept")
+                    nc.vector.tensor_mul(shared_of[blk, h][:], step2[:], share2_of[blk][:, head_columns(h)])
+                    continue
                 shared = narrow.tile([P, N], BF16, name="shared")
                 nc.vector.tensor_mul(shared[:], step2[:], share2_of[blk][:, head_columns(h)])
                 step1 = against_genes(blk, folded_query("step1", h), score_psum, "step1", "score")
-                nc.vector.tensor_add(mix_of[blk][:, head_columns(h)], step1[:], shared[:])
+                mix_of[blk, h] = mixes.tile([P, N], BF16, name="mix")
+                nc.vector.tensor_add(mix_of[blk, h][:], step1[:], shared[:])
+
+        def mix_in_psum(blk):
+            for h in range(H):
+                if tensor_mixes(h):
+                    mix_of[blk, h] = sum_psum.tile([P, N], BF16, name="mix_bank", tag="sum")
+                    for piece in range(PIECES):
+                        nc.tensor.matmul(
+                            mix_of[blk, h][:, piece_columns(piece)], genes(blk), folded_query("step1", h)[:, piece_columns(piece)],
+                            start=True, stop=False,
+                        )
+                        nc.tensor.matmul(
+                            mix_of[blk, h][:, piece_columns(piece)], identity[:], shared_of[blk, h][:, piece_columns(piece)],
+                            start=False, stop=True,
+                        )
 
         def logarithm(blk):
             nc.scalar.activation(lead_of[blk], share2_of[blk][:], LN, bias=floor[:, 0:1])
 
-        def tensor_subtracts(blk, h):
-            return h == 0 and blk % 2 == 1
-
         def find_lead(blk):
             for h in range(H):
-                if tensor_subtracts(blk, h):
-                    nc.vector.tensor_tensor(
-                        lead_of[blk][:, head_columns(h)], lead_of[blk][:, head_columns(h)], gap21_of[blk][:, head_columns(h)], MIN
-                    )
-                    continue
                 log_share = narrow.tile([P, N], BF16, name="log_share")
                 nc.vector.tensor_tensor(log_share[:], lead_of[blk][:, head_columns(h)], gap21_of[blk][:, head_columns(h)], MIN)
                 gap20 = against_genes(blk, folded_query("gap20", h), gap_psum, "gap20", "gap")
@@ -229,42 +239,38 @@ def tile_multiheadefralayer_nomp_b_kernel(
         def second_sigmoid(blk):
             both_of[blk] = wide.tile([P, H * N], BF16, name="both")
             for h in range(H):
-                lead = lead_of[blk][:, head_columns(h)]
-                if tensor_subtracts(blk, h):
-                    lead_bank = lead_psum.tile([P, N], BF16, name="lead_bank")
-                    for piece in range(PIECES):
-                        nc.tensor.matmul(
-                            lead_bank[:, piece_columns(piece)], genes(blk), folded_query("gap20", h)[:, piece_columns(piece)],
-                            start=True, stop=False,
-                        )
-                        nc.tensor.matmul(
-                            lead_bank[:, piece_columns(piece)], minus_identity[:], lead[:, piece_columns(piece)], start=False, stop=True
-                        )
-                    lead = lead_bank[:]
-                nc.scalar.activation(both_of[blk][:, head_columns(h)], lead, SIGMOID, bias=gap_bias["gap20"][:, h : h + 1])
+                nc.scalar.activation(
+                    both_of[blk][:, head_columns(h)], lead_of[blk][:, head_columns(h)], SIGMOID, bias=gap_bias["gap20"][:, h : h + 1]
+                )
 
         def find_gain(blk):
             gain_of[blk] = wide.tile([P, H * N], BF16, name="gain")
-            nc.vector.tensor_mul(gain_of[blk][:], both_of[blk][:], mix_of[blk][:])
+            for h in range(H):
+                nc.vector.tensor_mul(gain_of[blk][:, head_columns(h)], mix_of[blk, h][:], both_of[blk][:, head_columns(h)])
+
+        def scalar_copies(blk, piece):
+            return piece == 1 and blk % 2 == 1
 
         def sum_up(blk):
             totals_of[blk] = sum_psum.tile([P, N], BF16, name="total", tag="sum")
             for piece in range(PIECES):
                 total = totals_of[blk][:, piece_columns(piece)]
+                heads_summed_here = H if scalar_copies(blk, piece) else H - 1
                 nc.tensor.matmul(total, genes(blk), folded_first()[:, piece_columns(piece)], start=True, stop=False)
-                for h in range(H):
+                for h in range(heads_summed_here):
                     nc.tensor.matmul(
                         total, identity[:], gain_of[blk][:, h * N + piece * PIECE : h * N + (piece + 1) * PIECE],
-                        start=False, stop=(h == H - 1),
+                        start=False, stop=(h == heads_summed_here - 1),
                     )
 
         def store(blk):
             result = results.tile([P, N], F32, name="result")
             for piece in range(PIECES):
-                if piece == 1 and blk % 2 == 1:
+                if scalar_copies(blk, piece):
                     nc.scalar.copy(result[:, piece_columns(piece)], totals_of[blk][:, piece_columns(piece)])
                 else:
-                    nc.vector.tensor_copy(result[:, piece_columns(piece)], totals_of[blk][:, piece_columns(piece)])
+                    last_gain = gain_of[blk][:, (H - 1) * N + piece * PIECE : (H - 1) * N + (piece + 1) * PIECE]
+                    nc.vector.tensor_add(result[:, piece_columns(piece)], totals_of[blk][:, piece_columns(piece)], last_gain)
             nc.sync.dma_start(out[blk * P : (blk + 1) * P, :], result[:])
 
         batches = []
@@ -289,6 +295,7 @@ def tile_multiheadefralayer_nomp_b_kernel(
                 find_lead(blk)
             for blk in following:
                 keep_gap21(blk)
+            mix_in_psum(batch[0])
             for i in range(max(len(batch), len(following))):
                 if i < len(batch):
                     second_sigmoid(batch[i])
@@ -296,6 +303,8 @@ def tile_multiheadefralayer_nomp_b_kernel(
                     first_sigmoid(following[i])
                 if i < len(batch):
                     find_gain(batch[i])
+                if i + 1 < len(batch):
+                    mix_in_psum(batch[i + 1])
                 if i < len(following):
                     mix_scores(following[i])
                 if 1 <= i <= len(batch):

@@ -20,6 +20,7 @@ BF16, F32, U16 = mybir.dt.bfloat16, mybir.dt.float32, mybir.dt.uint16
 MULT, MIN = mybir.AluOpType.mult, mybir.AluOpType.min
 SIGMOID = mybir.ActivationFunctionType.Sigmoid
 LN = mybir.ActivationFunctionType.Ln
+COPY = mybir.ActivationFunctionType.Copy
 
 GAPS = {"gap21": (2, 1), "gap20": (2, 0)}
 
@@ -43,13 +44,14 @@ def tile_multiheadefralayer_nomp_b_kernel(
         tc.tile_pool(name="kept_gaps", bufs=LARGEST + 1) as kept_gaps,
         tc.tile_pool(name="shares", bufs=LARGEST + 1) as shares,
         tc.tile_pool(name="mixes", bufs=LARGEST + 1) as mixes,
+        tc.tile_pool(name="floors", bufs=2) as floors,
         tc.tile_pool(name="leads", bufs=1) as leads,
         tc.tile_pool(name="wide", bufs=3) as wide,
         tc.tile_pool(name="narrow", bufs=3) as narrow,
         tc.tile_pool(name="results", bufs=4) as results,
-        tc.psum_pool(name="gap_psum", bufs=3) as gap_psum,
-        tc.psum_pool(name="score_psum", bufs=2) as score_psum,
-        tc.psum_pool(name="sum_psum", bufs=3) as sum_psum,
+        tc.psum_pool(name="gap_psum", bufs=2) as gap_psum,
+        tc.psum_pool(name="score_psum", bufs=1) as score_psum,
+        tc.psum_pool(name="sum_psum", bufs=5) as sum_psum,
     ):
         identity = held.tile([P, P], BF16, name="identity")
         make_identity(nc, identity[:])
@@ -73,9 +75,6 @@ def tile_multiheadefralayer_nomp_b_kernel(
         nc.scalar.dma_start(gate[:], gate_w.rearrange("h e f -> (h e f)").partition_broadcast(P))
         gate_shift = held.tile([P, H * E], F32, name="gate_shift")
         nc.scalar.dma_start(gate_shift[:], gate_b.rearrange("h f -> (h f)").partition_broadcast(P))
-
-        floor = held.tile([P, 1], F32, name="floor")
-        nc.vector.memset(floor[:], FLOOR)
 
         gate_by_f = gate[:].rearrange("p (a f) -> p a f", f=E)
         shift_by_f = gate_shift[:].rearrange("p (h f) -> p h f", f=E)
@@ -112,10 +111,7 @@ def tile_multiheadefralayer_nomp_b_kernel(
         for h in range(H):
             for e in range(E):
                 for piece in range(PIECES):
-                    if turn % 2 == 0:
-                        projected = sum_psum.tile([DK, PIECE], F32, name="projected", tag="sum")
-                    else:
-                        projected = gap_psum.tile([DK, PIECE], F32, name="projected", tag="gap")
+                    projected = sum_psum.tile([DK, PIECE], F32, name="projected", tag="sum")
                     looked_up = table[:].indirect(offsets[:, piece * (PIECE // 16) : (piece + 1) * (PIECE // 16)])
                     nc.tensor.matmul(projected[:], wq[e][:, h * DK : (h + 1) * DK], looked_up, start=True, stop=True)
                     if turn % 2 == 0:
@@ -172,7 +168,7 @@ def tile_multiheadefralayer_nomp_b_kernel(
                 nc.vector.tensor_add(folds["first_fold"][:], folded_query("part0", 0)[:], folded_query("part0", 1)[:])
             return folds["first_fold"]
 
-        gap21_of, share2_of, shared_of, mix_of, lead_of, both_of, gain_of, totals_of = {}, {}, {}, {}, {}, {}, {}, {}
+        gap21_of, share2_of, kept_of, mix_of, lead_of, both_of, gain_of, totals_of = {}, {}, {}, {}, {}, {}, {}, {}
 
         def genes(blk):
             return table[:, blk * P : (blk + 1) * P]
@@ -196,37 +192,38 @@ def tile_multiheadefralayer_nomp_b_kernel(
             for h in range(H):
                 nc.scalar.activation(share2_of[blk][:, head_columns(h)], gap21_of[blk][:, head_columns(h)], SIGMOID)
 
-        def tensor_mixes(h):
-            return h == 0
+        def tensor_mixes(blk, h):
+            return h == 0 or blk % 2 == 0
 
         def mix_scores(blk):
+            kept_of[blk] = mixes.tile([P, H * N], BF16, name="kept")
             for h in range(H):
                 step2 = against_genes(blk, folded_query("step2", h), score_psum, "step2", "score")
-                if tensor_mixes(h):
-                    shared_of[blk, h] = mixes.tile([P, N], BF16, name="shared_kept")
-                    nc.vector.tensor_mul(shared_of[blk, h][:], step2[:], share2_of[blk][:, head_columns(h)])
+                if tensor_mixes(blk, h):
+                    nc.vector.tensor_mul(kept_of[blk][:, head_columns(h)], step2[:], share2_of[blk][:, head_columns(h)])
                     continue
                 shared = narrow.tile([P, N], BF16, name="shared")
                 nc.vector.tensor_mul(shared[:], step2[:], share2_of[blk][:, head_columns(h)])
                 step1 = against_genes(blk, folded_query("step1", h), score_psum, "step1", "score")
-                mix_of[blk, h] = mixes.tile([P, N], BF16, name="mix")
-                nc.vector.tensor_add(mix_of[blk, h][:], step1[:], shared[:])
+                nc.vector.tensor_add(kept_of[blk][:, head_columns(h)], step1[:], shared[:])
+                mix_of[blk, h] = kept_of[blk][:, head_columns(h)]
 
         def mix_in_psum(blk):
             for h in range(H):
-                if tensor_mixes(h):
-                    mix_of[blk, h] = sum_psum.tile([P, N], BF16, name="mix_bank", tag="sum")
+                if tensor_mixes(blk, h):
+                    mix_bank = sum_psum.tile([P, N], BF16, name="mix_bank", tag="sum")
                     for piece in range(PIECES):
                         nc.tensor.matmul(
-                            mix_of[blk, h][:, piece_columns(piece)], genes(blk), folded_query("step1", h)[:, piece_columns(piece)],
+                            mix_bank[:, piece_columns(piece)], genes(blk), folded_query("step1", h)[:, piece_columns(piece)],
                             start=True, stop=False,
                         )
                         nc.tensor.matmul(
-                            mix_of[blk, h][:, piece_columns(piece)], identity[:], shared_of[blk, h][:, piece_columns(piece)],
+                            mix_bank[:, piece_columns(piece)], identity[:], kept_of[blk][:, h * N + piece * PIECE : h * N + (piece + 1) * PIECE],
                             start=False, stop=True,
                         )
+                    mix_of[blk, h] = mix_bank[:]
 
-        def logarithm(blk):
+        def logarithm(blk, floor):
             nc.scalar.activation(lead_of[blk], share2_of[blk][:], LN, bias=floor[:, 0:1])
 
         def find_lead(blk):
@@ -246,31 +243,18 @@ def tile_multiheadefralayer_nomp_b_kernel(
         def find_gain(blk):
             gain_of[blk] = wide.tile([P, H * N], BF16, name="gain")
             for h in range(H):
-                nc.vector.tensor_mul(gain_of[blk][:, head_columns(h)], mix_of[blk, h][:], both_of[blk][:, head_columns(h)])
-
-        def scalar_copies(blk, piece):
-            return piece == 1 and blk % 2 == 1
+                nc.vector.tensor_mul(gain_of[blk][:, head_columns(h)], mix_of[blk, h], both_of[blk][:, head_columns(h)])
 
         def sum_up(blk):
             totals_of[blk] = sum_psum.tile([P, N], BF16, name="total", tag="sum")
             for piece in range(PIECES):
                 total = totals_of[blk][:, piece_columns(piece)]
-                heads_summed_here = H if scalar_copies(blk, piece) else H - 1
                 nc.tensor.matmul(total, genes(blk), folded_first()[:, piece_columns(piece)], start=True, stop=False)
-                for h in range(heads_summed_here):
-                    nc.tensor.matmul(
-                        total, identity[:], gain_of[blk][:, h * N + piece * PIECE : h * N + (piece + 1) * PIECE],
-                        start=False, stop=(h == heads_summed_here - 1),
-                    )
+                nc.tensor.matmul(total, identity[:], gain_of[blk][:, piece_columns(piece)], start=False, stop=True)
 
         def store(blk):
             result = results.tile([P, N], F32, name="result")
-            for piece in range(PIECES):
-                if scalar_copies(blk, piece):
-                    nc.scalar.copy(result[:, piece_columns(piece)], totals_of[blk][:, piece_columns(piece)])
-                else:
-                    last_gain = gain_of[blk][:, (H - 1) * N + piece * PIECE : (H - 1) * N + (piece + 1) * PIECE]
-                    nc.vector.tensor_add(result[:, piece_columns(piece)], totals_of[blk][:, piece_columns(piece)], last_gain)
+            nc.vector.tensor_add(result[:], totals_of[blk][:], gain_of[blk][:, head_columns(1)])
             nc.sync.dma_start(out[blk * P : (blk + 1) * P, :], result[:])
 
         batches = []
@@ -289,8 +273,10 @@ def tile_multiheadefralayer_nomp_b_kernel(
             leads_of_batch = leads.tile([P, len(batch) * H * N], BF16, name="leads_of_batch")
             for i, blk in enumerate(batch):
                 lead_of[blk] = leads_of_batch[:, i * H * N : (i + 1) * H * N]
-            for blk in batch[-1:] + batch[:-1]:
-                logarithm(blk)
+            floor = floors.tile([P, 1], F32, name="floor")
+            nc.scalar.activation(floor[:], share2_of[batch[-1]][:, H * N - 1 : H * N], COPY, bias=FLOOR, scale=0.0)
+            for blk in batch:
+                logarithm(blk, floor)
             for blk in batch:
                 find_lead(blk)
             for blk in following:

@@ -246,7 +246,10 @@ def tile_multiheadefralayer_nomp_b_kernel(
                 nc.vector.tensor_mul(gain_of[blk][:, head_columns(h)], mix_of[blk, h], both_of[blk][:, head_columns(h)])
 
         def sum_up(blk):
-            totals_of[blk] = sum_psum.tile([P, N], BF16, name="total", tag="sum")
+            if blk in batches[-1]:
+                totals_of[blk] = gap_psum.tile([P, N], BF16, name="late_total", tag="gap")
+            else:
+                totals_of[blk] = sum_psum.tile([P, N], BF16, name="total", tag="sum")
             for piece in range(PIECES):
                 total = totals_of[blk][:, piece_columns(piece)]
                 nc.tensor.matmul(total, genes(blk), folded_first()[:, piece_columns(piece)], start=True, stop=False)
@@ -281,7 +284,9 @@ def tile_multiheadefralayer_nomp_b_kernel(
                 find_lead(blk)
             for blk in following:
                 keep_gap21(blk)
-            mix_in_psum(batch[0])
+            ahead = batch[:1] if following else batch
+            for blk in ahead:
+                mix_in_psum(blk)
             for i in range(max(len(batch), len(following))):
                 if i < len(batch):
                     second_sigmoid(batch[i])
@@ -289,7 +294,7 @@ def tile_multiheadefralayer_nomp_b_kernel(
                     first_sigmoid(following[i])
                 if i < len(batch):
                     find_gain(batch[i])
-                if i + 1 < len(batch):
+                if i + 1 < len(batch) and batch[i + 1] not in ahead:
                     mix_in_psum(batch[i + 1])
                 if i < len(following):
                     mix_scores(following[i])

@@ -12,6 +12,7 @@ BANK_BF16 = 1024
 BATCHES = (5, 6, 5)
 assert sum(BATCHES) == BLOCKS
 LARGEST = max(BATCHES)
+SCALAR_STORES = (BLOCKS - 3, BLOCKS - 2)
 FLOOR = 2.0 ** -64
 
 FLOPS = 2 * (N + S) * D * H * DK * E + 2 * S * N * DK * H * E
@@ -246,18 +247,30 @@ def tile_multiheadefralayer_nomp_b_kernel(
                 nc.vector.tensor_mul(gain_of[blk][:, head_columns(h)], mix_of[blk, h], both_of[blk][:, head_columns(h)])
 
         def sum_up(blk):
-            if blk in batches[-1]:
+            if blk == SCALAR_STORES[0]:
+                totals_of[blk] = score_psum.tile([P, N], BF16, name="waiting_total", tag="score")
+            elif blk in batches[-1]:
                 totals_of[blk] = gap_psum.tile([P, N], BF16, name="late_total", tag="gap")
             else:
                 totals_of[blk] = sum_psum.tile([P, N], BF16, name="total", tag="sum")
+            heads_added = H if blk in SCALAR_STORES else 1
             for piece in range(PIECES):
                 total = totals_of[blk][:, piece_columns(piece)]
                 nc.tensor.matmul(total, genes(blk), folded_first()[:, piece_columns(piece)], start=True, stop=False)
-                nc.tensor.matmul(total, identity[:], gain_of[blk][:, piece_columns(piece)], start=False, stop=True)
+                for h in range(heads_added):
+                    nc.tensor.matmul(
+                        total, identity[:], gain_of[blk][:, h * N + piece * PIECE : h * N + (piece + 1) * PIECE],
+                        start=False, stop=(h == heads_added - 1),
+                    )
 
         def store(blk):
             result = results.tile([P, N], F32, name="result")
             nc.vector.tensor_add(result[:], totals_of[blk][:], gain_of[blk][:, head_columns(1)])
+            nc.sync.dma_start(out[blk * P : (blk + 1) * P, :], result[:])
+
+        def scalar_stores(blk):
+            result = results.tile([P, N], F32, name="result")
+            nc.scalar.copy(result[:], totals_of[blk][:])
             nc.sync.dma_start(out[blk * P : (blk + 1) * P, :], result[:])
 
         batches = []
@@ -298,9 +311,12 @@ def tile_multiheadefralayer_nomp_b_kernel(
                     mix_in_psum(batch[i + 1])
                 if i < len(following):
                     mix_scores(following[i])
-                if 1 <= i <= len(batch):
+                if 1 <= i <= len(batch) and batch[i - 1] not in SCALAR_STORES:
                     store(batch[i - 1])
                 if i < len(batch):
                     sum_up(batch[i])
+            if not following:
+                for blk in SCALAR_STORES:
+                    scalar_stores(blk)
             if len(batch) >= len(following):
                 store(batch[-1])

@@ -228,11 +228,11 @@ def tile_multiheadefralayer_nomp_b_kernel(
             nc.scalar.activation(lead_of[blk], share2_of[blk][:], LN, bias=floor[:, 0:1])
 
         def find_lead(blk):
+            log_share = wide.tile([P, H * N], BF16, name="log_share")
+            nc.vector.tensor_tensor(log_share[:], lead_of[blk], gap21_of[blk][:], MIN)
             for h in range(H):
-                log_share = narrow.tile([P, N], BF16, name="log_share")
-                nc.vector.tensor_tensor(log_share[:], lead_of[blk][:, head_columns(h)], gap21_of[blk][:, head_columns(h)], MIN)
                 gap20 = against_genes(blk, folded_query("gap20", h), gap_psum, "gap20", "gap")
-                nc.vector.tensor_sub(lead_of[blk][:, head_columns(h)], gap20[:], log_share[:])
+                nc.vector.tensor_sub(lead_of[blk][:, head_columns(h)], gap20[:], log_share[:, head_columns(h)])
 
         def second_sigmoid(blk):
             both_of[blk] = wide.tile([P, H * N], BF16, name="both")

@@ -190,8 +190,11 @@ def tile_multiheadefralayer_nomp_b_kernel(
 
         def first_sigmoid(blk):
             share2_of[blk] = shares.tile([P, H * N], BF16, name="share2")
-            for h in range(H):
-                nc.scalar.activation(share2_of[blk][:, head_columns(h)], gap21_of[blk][:, head_columns(h)], SIGMOID)
+            if blk in batches[0]:
+                for h in range(H):
+                    nc.scalar.activation(share2_of[blk][:, head_columns(h)], gap21_of[blk][:, head_columns(h)], SIGMOID)
+            else:
+                nc.scalar.activation(share2_of[blk][:], gap21_of[blk][:], SIGMOID)
 
         def tensor_mixes(blk, h):
             return h == 0 or blk % 2 == 0

@@ -77,6 +77,9 @@ def tile_multiheadefralayer_nomp_b_kernel(
         gate_shift = held.tile([P, H * E], F32, name="gate_shift")
         nc.scalar.dma_start(gate_shift[:], gate_b.rearrange("h f -> (h f)").partition_broadcast(P))
 
+        warmed = held.tile([P, 1], F32, name="warmed")
+        nc.scalar.activation(warmed[:], identity[:, 0:1], SIGMOID)
+
         gate_by_f = gate[:].rearrange("p (a f) -> p a f", f=E)
         shift_by_f = gate_shift[:].rearrange("p (h f) -> p h f", f=E)
         gap_weight, gap_bias = {}, {}

import math

import concourse.mybir as mybir
from concourse.masks import make_identity

S, D, H, DK, E, N = 2048, 128, 2, 128, 3, 1024
P = 128
BLOCKS = S // P
PIECE = 512
PIECES = N // PIECE
BANK_BF16 = 1024
BATCHES = (5, 6, 5)
assert sum(BATCHES) == BLOCKS
LARGEST = max(BATCHES)
SCALAR_STORES = (BLOCKS - 3, BLOCKS - 2)
FLOOR = 2.0 ** -64

FLOPS = 2 * (N + S) * D * H * DK * E + 2 * S * N * DK * H * E

BF16, F32, U16 = mybir.dt.bfloat16, mybir.dt.float32, mybir.dt.uint16
MULT, MIN = mybir.AluOpType.mult, mybir.AluOpType.min
SIGMOID = mybir.ActivationFunctionType.Sigmoid
LN = mybir.ActivationFunctionType.Ln
COPY = mybir.ActivationFunctionType.Copy

GAPS = {"gap21": (2, 1), "gap20": (2, 0)}


def piece_columns(piece):
    return slice(piece * PIECE, (piece + 1) * PIECE)


def head_columns(h):
    return slice(h * N, (h + 1) * N)


def tile_multiheadefralayer_nomp_b_kernel(
    tc, z, wq_seq, wk_seq, wq_exp, wk_exp, wq_txt, wk_txt, gate_w, gate_b, offs, out
):
    nc = tc.nc
    inv_sqrt_dk = 1.0 / math.sqrt(DK)

    with (
        tc.tile_pool(name="held", bufs=1) as held,
        tc.tile_pool(name="kept_gaps", bufs=LARGEST + 1) as kept_gaps,
        tc.tile_pool(name="shares", bufs=LARGEST + 1) as shares,
        tc.tile_pool(name="mixes", bufs=LARGEST + 1) as mixes,
        tc.tile_pool(name="floors", bufs=2) as floors,
        tc.tile_pool(name="leads", bufs=1) as leads,
        tc.tile_pool(name="wide", bufs=3) as wide,
        tc.tile_pool(name="narrow", bufs=3) as narrow,
        tc.tile_pool(name="results", bufs=4) as results,
        tc.psum_pool(name="gap_psum", bufs=2) as gap_psum,
        tc.psum_pool(name="score_psum", bufs=1) as score_psum,
        tc.psum_pool(name="sum_psum", bufs=5) as sum_psum,
    ):
        identity = held.tile([P, P], BF16, name="identity")
        make_identity(nc, identity[:])

        offsets = held.tile([P, N // 16], U16, name="offsets")
        nc.sync.dma_start(offsets[:], offs)

        z_rows = held.tile([P, BLOCKS, D], BF16, name="z_rows")
        z_blocks = z.rearrange("(b p) c -> p b c", p=P)
        quarter = BLOCKS // 4
        for i in range(4):
            nc.sync.dma_start(z_rows[:, i * quarter : (i + 1) * quarter, :], z_blocks[:, i * quarter : (i + 1) * quarter, :])

        wq = [held.tile([D, H * DK], BF16, name=f"wq{e}") for e in range(E)]
        wk = [held.tile([D, H * DK], BF16, name=f"wk{e}") for e in range(E)]
        for e, (wq_dram, wk_dram) in enumerate(((wq_seq, wk_seq), (wq_exp, wk_exp), (wq_txt, wk_txt))):
            nc.sync.dma_start(wq[e][:], wq_dram)
            nc.scalar.dma_start(wk[e][:], wk_dram)

        gate = held.tile([P, H * E * E], F32, name="gate")
        nc.scalar.dma_start(gate[:], gate_w.rearrange("h e f -> (h e f)").partition_broadcast(P))
        gate_shift = held.tile([P, H * E], F32, name="gate_shift")
        nc.scalar.dma_start(gate_shift[:], gate_b.rearrange("h f -> (h f)").partition_broadcast(P))

        warmed = held.tile([P, 1], F32, name="warmed")
        nc.scalar.activation(warmed[:], identity[:, 0:1], SIGMOID)

        gate_by_f = gate[:].rearrange("p (a f) -> p a f", f=E)
        shift_by_f = gate_shift[:].rearrange("p (h f) -> p h f", f=E)
        gap_weight, gap_bias = {}, {}
        for kind, (high, low) in GAPS.items():
            gap_weight[kind] = held.tile([P, H * E], F32, name=f"{kind}_weight")
            nc.vector.tensor_sub(gap_weight[kind][:], gate_by_f[:, :, high], gate_by_f[:, :, low])
            gap_bias[kind] = held.tile([P, H], F32, name=f"{kind}_bias")
            nc.vector.tensor_sub(gap_bias[kind][:], shift_by_f[:, :, high], shift_by_f[:, :, low])

        table = held.tile([D, S], BF16, name="table")
        per_bank = BANK_BF16 // P
        for bank in range(BLOCKS // per_bank):
            z_flipped = gap_psum.tile([D, BANK_BF16], BF16, name="z_flipped", tag="gap")
            for i in range(per_bank):
                nc.tensor.transpose(z_flipped[:, i * P : (i + 1) * P], z_rows[:, bank * per_bank + i, :], identity[:])
            if bank % 2 == 0:
                nc.vector.tensor_copy(table[:, bank * BANK_BF16 : (bank + 1) * BANK_BF16], z_flipped[:])
            else:
                nc.scalar.copy(table[:, bank * BANK_BF16 : (bank + 1) * BANK_BF16], z_flipped[:])

        def wk_columns(e, h):
            return slice((e * H + h) * D, (e * H + h + 1) * D)

        wk_flipped = score_psum.tile([DK, E * H * D], BF16, name="wk_flipped", tag="score")
        for e in range(E):
            for h in range(H):
                nc.tensor.transpose(wk_flipped[:, wk_columns(e, h)], wk[e][:, h * DK : (h + 1) * DK], identity[:])
        wk_t = held.tile([DK, E * H * D], BF16, name="wk_t")
        nc.vector.tensor_copy(wk_t[:], wk_flipped[:])

        qry = [[held.tile([DK, N], BF16, name=f"qry{e}{h}") for h in range(H)] for e in range(E)]
        turn = 0
        for h in range(H):
            for e in range(E):
                for piece in range(PIECES):
                    projected = sum_psum.tile([DK, PIECE], F32, name="projected", tag="sum")
                    looked_up = table[:].indirect(offsets[:, piece * (PIECE // 16) : (piece + 1) * (PIECE // 16)])
                    nc.tensor.matmul(projected[:], wq[e][:, h * DK : (h + 1) * DK], looked_up, start=True, stop=True)
                    if turn % 2 == 0:
                        nc.vector.tensor_copy(qry[e][h][:, piece_columns(piece)], projected[:])
                    else:
                        nc.scalar.copy(qry[e][h][:, piece_columns(piece)], projected[:])
                    turn += 1

        def fold(name, terms):
            folded = held.tile([D, N], BF16, name=name)
            summed = sum_psum.tile([D, N], BF16, name="summed", tag="sum")
            for piece in range(PIECES):
                for i, (scaled_keys, queries) in enumerate(terms):
                    nc.tensor.matmul(
                        summed[:, piece_columns(piece)], scaled_keys, queries[:, piece_columns(piece)],
                        start=(i == 0), stop=(i == len(terms) - 1),
                    )
            nc.vector.tensor_copy(folded[:], summed[:])
            return folded

        part_keys = held.tile([DK, E * H * D], BF16, name="part_keys")
        nc.vector.tensor_scalar_mul(part_keys[:], wk_t[:], inv_sqrt_dk / H)

        def gated(h, kind):
            terms = []
            for e in range(E):
                scaled_keys = held.tile([DK, D], BF16, name=f"{kind}_keys{h}{e}")
                gate_difference = gap_weight[kind][:, h * E + e : h * E + e + 1]
                nc.vector.tensor_scalar(scaled_keys[:], wk_t[:, wk_columns(e, h)], gate_difference, inv_sqrt_dk, MULT, MULT)
                terms.append((scaled_keys[:], qry[e][h]))
            return terms

        folds = {}

        def folded_query(kind, h):
            name = f"{kind}_fold{h}"
            if name not in folds:
                if kind == "step1":
                    folds[name] = held.tile([D, N], BF16, name=name)
                    nc.vector.tensor_sub(folds[name][:], folded_query("part1", h)[:], folded_query("part0", h)[:])
                elif kind == "step2":
                    folds[name] = held.tile([D, N], BF16, name=name)
                    nc.vector.tensor_sub(folds[name][:], folded_query("part2", h)[:], folded_query("part1", h)[:])
                elif kind.startswith("part"):
                    e = int(kind[-1])
                    folds[name] = fold(name, [(part_keys[:, wk_columns(e, h)], qry[e][h])])
                else:
                    folds[name] = fold(name, gated(h, kind))
            return folds[name]

        def folded_first():
            if "first_fold" not in folds:
                folds["first_fold"] = held.tile([D, N], BF16, name="first_fold")
                nc.vector.tensor_add(folds["first_fold"][:], folded_query("part0", 0)[:], folded_query("part0", 1)[:])
            return folds["first_fold"]

        gap21_of, share2_of, kept_of, mix_of, lead_of, both_of, gain_of, totals_of = {}, {}, {}, {}, {}, {}, {}, {}

        def genes(blk):
            return table[:, blk * P : (blk + 1) * P]

        def against_genes(blk, folded, pool, name, tag):
            bank = pool.tile([P, N], BF16, name=name, tag=tag)
            for piece in range(PIECES):
                nc.tensor.matmul(
                    bank[:, piece_columns(piece)], genes(blk), folded[:, piece_columns(piece)], start=True, stop=True
                )
            return bank

        def keep_gap21(blk):
            gap21_of[blk] = kept_gaps.tile([P, H * N], BF16, name="gap21_kept")
            for h in range(H):
                gap21 = against_genes(blk, folded_query("gap21", h), gap_psum, "gap21", "gap")
                nc.vector.tensor_scalar_add(gap21_of[blk][:, head_columns(h)], gap21[:], gap_bias["gap21"][:, h : h + 1])

        def first_sigmoid(blk):
            share2_of[blk] = shares.tile([P, H * N], BF16, name="share2")
            if blk in batches[0]:
                for h in range(H):
                    nc.scalar.activation(share2_of[blk][:, head_columns(h)], gap21_of[blk][:, head_columns(h)], SIGMOID)
            else:
                nc.scalar.activation(share2_of[blk][:], gap21_of[blk][:], SIGMOID)

        def tensor_mixes(blk, h):
            return h == 0 or blk % 2 == 0

        def mix_scores(blk):
            kept_of[blk] = mixes.tile([P, H * N], BF16, name="kept")
            for h in range(H):
                step2 = against_genes(blk, folded_query("step2", h), score_psum, "step2", "score")
                if tensor_mixes(blk, h):
                    nc.vector.tensor_mul(kept_of[blk][:, head_columns(h)], step2[:], share2_of[blk][:, head_columns(h)])
                    continue
                shared = narrow.tile([P, N], BF16, name="shared")
                nc.vector.tensor_mul(shared[:], step2[:], share2_of[blk][:, head_columns(h)])
                step1 = against_genes(blk, folded_query("step1", h), score_psum, "step1", "score")
                nc.vector.tensor_add(kept_of[blk][:, head_columns(h)], step1[:], shared[:])
                mix_of[blk, h] = kept_of[blk][:, head_columns(h)]

        def mix_in_psum(blk):
            for h in range(H):
                if tensor_mixes(blk, h):
                    mix_bank = sum_psum.tile([P, N], BF16, name="mix_bank", tag="sum")
                    for piece in range(PIECES):
                        nc.tensor.matmul(
                            mix_bank[:, piece_columns(piece)], genes(blk), folded_query("step1", h)[:, piece_columns(piece)],
                            start=True, stop=False,
                        )
                        nc.tensor.matmul(
                            mix_bank[:, piece_columns(piece)], identity[:], kept_of[blk][:, h * N + piece * PIECE : h * N + (piece + 1) * PIECE],
                            start=False, stop=True,
                        )
                    mix_of[blk, h] = mix_bank[:]

        def logarithm(blk, floor):
            nc.scalar.activation(lead_of[blk], share2_of[blk][:], LN, bias=floor[:, 0:1])

        def find_lead(blk):
            log_share = wide.tile([P, H * N], BF16, name="log_share")
            nc.vector.tensor_tensor(log_share[:], lead_of[blk], gap21_of[blk][:], MIN)
            for h in range(H):
                gap20 = against_genes(blk, folded_query("gap20", h), gap_psum, "gap20", "gap")
                nc.vector.tensor_sub(lead_of[blk][:, head_columns(h)], gap20[:], log_share[:, head_columns(h)])

        def second_sigmoid(blk):
            both_of[blk] = wide.tile([P, H * N], BF16, name="both")
            for h in range(H):
                nc.scalar.activation(
                    both_of[blk][:, head_columns(h)], lead_of[blk][:, head_columns(h)], SIGMOID, bias=gap_bias["gap20"][:, h : h + 1]
                )

        def find_gain(blk):
            gain_of[blk] = wide.tile([P, H * N], BF16, name="gain")
            for h in range(H):
                nc.vector.tensor_mul(gain_of[blk][:, head_columns(h)], mix_of[blk, h], both_of[blk][:, head_columns(h)])

        def sum_up(blk):
            if blk == SCALAR_STORES[0]:
                totals_of[blk] = score_psum.tile([P, N], BF16, name="waiting_total", tag="score")
            elif blk in batches[-1]:
                totals_of[blk] = gap_psum.tile([P, N], BF16, name="late_total", tag="gap")
            else:
                totals_of[blk] = sum_psum.tile([P, N], BF16, name="total", tag="sum")
            heads_added = H if blk in SCALAR_STORES else 1
            for piece in range(PIECES):
                total = totals_of[blk][:, piece_columns(piece)]
                nc.tensor.matmul(total, genes(blk), folded_first()[:, piece_columns(piece)], start=True, stop=False)
                for h in range(heads_added):
                    nc.tensor.matmul(
                        total, identity[:], gain_of[blk][:, h * N + piece * PIECE : h * N + (piece + 1) * PIECE],
                        start=False, stop=(h == heads_added - 1),
                    )

        def store(blk):
            result = results.tile([P, N], F32, name="result")
            nc.vector.tensor_add(result[:], totals_of[blk][:], gain_of[blk][:, head_columns(1)])
            nc.sync.dma_start(out[blk * P : (blk + 1) * P, :], result[:])

        def scalar_stores(blk):
            result = results.tile([P, N], F32, name="result")
            nc.scalar.copy(result[:], totals_of[blk][:])
            nc.sync.dma_start(out[blk * P : (blk + 1) * P, :], result[:])

        batches = []
        for size in BATCHES:
            start = sum(len(batch) for batch in batches)
            batches.append(list(range(start, start + size)))

        for blk in batches[0]:
            keep_gap21(blk)
            first_sigmoid(blk)
        for blk in batches[0]:
            mix_scores(blk)

        for k, batch in enumerate(batches):
            following = batches[k + 1] if k + 1 < len(batches) else []
            leads_of_batch = leads.tile([P, len(batch) * H * N], BF16, name="leads_of_batch")
            for i, blk in enumerate(batch):
                lead_of[blk] = leads_of_batch[:, i * H * N : (i + 1) * H * N]
            floor = floors.tile([P, 1], F32, name="floor")
            nc.scalar.activation(floor[:], share2_of[batch[-1]][:, H * N - 1 : H * N], COPY, bias=FLOOR, scale=0.0)
            for blk in batch:
                logarithm(blk, floor)
            for blk in batch:
                find_lead(blk)
            for blk in following:
                keep_gap21(blk)
            ahead = batch[:1] if following else batch
            for blk in ahead:
                mix_in_psum(blk)
            for i in range(max(len(batch), len(following))):
                if i < len(batch):
                    second_sigmoid(batch[i])
                if i < len(following):
                    first_sigmoid(following[i])
                if i < len(batch):
                    find_gain(batch[i])
                if i + 1 < len(batch) and batch[i + 1] not in ahead:
                    mix_in_psum(batch[i + 1])
                if i < len(following):
                    mix_scores(following[i])
                if 1 <= i <= len(batch) and batch[i - 1] not in SCALAR_STORES:
                    store(batch[i - 1])
                if i < len(batch):
                    sum_up(batch[i])
            if not following:
                for blk in SCALAR_STORES:
                    scalar_stores(blk)
            if len(batch) >= len(following):
                store(batch[-1])
